import numpy as np
import ml_dtypes


def mxq(x, axis, fmt="e4m3"):
    dtype, down = {"e4m3": (ml_dtypes.float8_e4m3fn, 7), "e5m2": (ml_dtypes.float8_e5m2, 14)}[fmt]
    v = np.moveaxis(np.asarray(x, np.float32).astype(ml_dtypes.bfloat16).astype(np.float64), axis, -1)
    blocks = v.reshape(v.shape[:-1] + (-1, 32))
    amax = np.abs(blocks).max(-1, keepdims=True)
    byte = np.maximum(np.where(amax > 0, np.frexp(amax)[1] - 1 + 127, 0) - down, 1)
    scale = np.exp2(byte - 127.0)
    codes = (blocks / scale).astype(np.float32).astype(dtype).astype(np.float64)
    return np.moveaxis((codes * scale).reshape(v.shape), -1, axis)


WIDE = False


def mx_kscale(k):
    if not WIDE:
        return np.ones(k)
    levels = np.array([10, -10, 5, -5, 0])
    a = np.random.permutation(np.resize(levels, k // 512 * 4)).reshape(k // 512, 4)
    idx = np.arange(k)
    return np.exp2(a[idx // 512, idx % 128 // 32])


BF16 = ml_dtypes.bfloat16


def bf(x):
    return np.asarray(x, np.float32).astype(BF16)


def f64(x):
    return np.asarray(x).astype(np.float64)


E2M1 = np.array([0.0, 0.5, 1.0, 1.5, 2.0, 3.0, 4.0, 6.0, -0.0, -0.5, -1.0, -1.5, -2.0, -3.0, -4.0, -6.0])


def pack_weight(w, fmt):
    k, n = w.shape
    w = f64(bf(w)).reshape(k // 32, 32, n)
    amax = np.abs(w).max(1)
    if fmt == "e4m3":
        byte = np.frexp(amax)[1] - 1 + 127 - 7
    else:
        mant, ex = np.frexp(amax / 6.0)
        byte = np.where(mant > 0.5, ex, ex - 1) + 127
    byte = np.clip(np.where(amax > 0, byte, 1), 1, 254)
    scaled = (w * np.exp2(127.0 - byte)[:, None, :]).reshape(k, n).astype(np.float32)
    by_word = np.ascontiguousarray(scaled.reshape(k // 512, 128, 4, n).transpose(0, 1, 3, 2))
    if fmt == "e4m3":
        words = by_word.astype(ml_dtypes.float8_e4m3fn).view(np.uint8)
    else:
        c = by_word.astype(ml_dtypes.float4_e2m1fn).view(np.uint8) & 0xF
        words = c[..., 0::2] | (c[..., 1::2] << 4)
    return np.ascontiguousarray(words), np.ascontiguousarray(byte.astype(np.uint8).reshape(k // 512, 16, n))


def unpack_weight(words, scales, fmt):
    g, p, n, _ = words.shape
    if fmt == "e4m3":
        vals = np.ascontiguousarray(words).view(ml_dtypes.float8_e4m3fn).astype(np.float64)
    else:
        nib = np.empty((g, p, n, 4), np.uint8)
        nib[..., 0::2] = words & 0xF
        nib[..., 1::2] = words >> 4
        vals = E2M1[nib]
    vals = vals * np.repeat(np.exp2(scales.astype(np.float64) - 127.0), 8, axis=1)[..., None]
    return vals.transpose(0, 1, 3, 2).reshape(g * 512, n)


N, D_IN, H0, H1, K = 1024, 3072, 1024, 256, 20
V = 1.0
FMT = "e4m3"


def silu(v):
    return v / (1.0 + np.exp(-v))


def setup_inputs():
    s = mx_kscale(D_IN)
    w1 = np.random.standard_normal((D_IN, H0)) / np.sqrt(D_IN)
    b1 = np.random.standard_normal(H0) * 0.2
    w2 = np.random.standard_normal((H0, H1)) * 4.0 / np.sqrt(H0 * H1)
    b2 = np.random.standard_normal(H1) * 0.1
    cent = np.random.standard_normal((K, D_IN)) * 0.9
    x = cent[np.random.randint(0, K, N)] + np.random.standard_normal((N, D_IN)) * 0.44
    hc = silu(np.stack([(c[:, None] * w1).sum(0) for c in cent]) + b1)
    clusters = (hc[:, :, None] * w2[None]).sum(1) + b2 + np.random.standard_normal((K, H1)) * 0.5 / np.sqrt(H1)
    W1_words, W1_scales = pack_weight(w1 / s[:, None], FMT)
    W2_words, W2_scales = pack_weight(w2, FMT)
    return {"x": bf(x * s), "W1_words": W1_words, "W1_scales": W1_scales, "b1": bf(b1), "W2_words": W2_words, "W2_scales": W2_scales, "b2": bf(b2), "clusters": bf(clusters)}


def reference(x, W1_words, W1_scales, b1, W2_words, W2_scales, b2, clusters):
    h = silu((mxq(f64(x), 1, "e4m3") @ unpack_weight(W1_words, W1_scales, FMT)) + f64(b1))
    z = (mxq(h, 1, "e4m3") @ unpack_weight(W2_words, W2_scales, FMT)) + f64(b2)
    d2 = np.stack([((z - c) ** 2).sum(1) for c in f64(clusters)], axis=1)
    q = 1.0 / (1.0 + d2 / V)
    q = q ** ((V + 1.0) / 2.0)
    q = q / q.sum(1, keepdims=True)
    return z, q

@@ -1,0 +1,318 @@
+from contextlib import ExitStack
+
+import concourse.mybir as mybir
+from concourse.masks import make_identity
+
+F32 = mybir.dt.float32
+BF16 = mybir.dt.bfloat16
+I32 = mybir.dt.int32
+U32 = mybir.dt.uint32
+U8 = mybir.dt.uint8
+FP8X4 = mybir.dt.float8_e4m3fn_x4
+ACT = mybir.ActivationFunctionType
+ALU = mybir.AluOpType
+AXIS = mybir.AxisListType
+
+P = 128
+PACK = 4
+K_PASS = P * PACK
+BANK = 512
+
+TOKENS, D_IN, H0, H1, CENTROIDS = 1024, 3072, 1024, 256, 20
+TILES = TOKENS // P
+PASSES_1 = D_IN // K_PASS
+PASSES_2 = H0 // K_PASS
+Z_HALVES = H1 // P
+CENTROIDS_PAD = 32
+FIRST_GROUP = 2
+
+FLOPS = 2 * TOKENS * D_IN * H0 + 2 * TOKENS * H0 * H1
+
+
+def tile_lintrans_pa_kernel(
+    tc, x, W1_words, W1_scales, b1, W2_words, W2_scales, b2, clusters, out_0, out_1
+):
+    nc = tc.nc
+    groups = [list(range(FIRST_GROUP))] + [[i] for i in range(FIRST_GROUP, TILES)]
+
+    def group(a):
+        return groups[a] if 0 <= a < len(groups) else []
+
+    x_tiles_dram = x.rearrange("(p i) k -> i p k", i=TILES)
+    z_tiles_dram = out_0.rearrange("(p i) j -> i p j", i=TILES)
+
+    with ExitStack() as ctx:
+        keep = ctx.enter_context(tc.tile_pool(name="keep", bufs=1))
+        x_pool = ctx.enter_context(tc.tile_pool(name="x_pool", bufs=TILES))
+        w1_pool = ctx.enter_context(tc.tile_pool(name="w1_pool", bufs=PASSES_1))
+        work = ctx.enter_context(tc.tile_pool(name="work", bufs=4))
+        ps_x = ctx.enter_context(tc.psum_pool(name="ps_x", bufs=3))
+        ps_h = ctx.enter_context(tc.psum_pool(name="ps_h", bufs=4))
+        ps_z = ctx.enter_context(tc.psum_pool(name="ps_z", bufs=1))
+        ctx.enter_context(tc.manual_schedule())
+
+        planes_a = keep.tile([P, H0], U8, align_bytes=64)
+        planes_b = keep.tile([P, H0], U8, align_bytes=64)
+        nc.vector.memset(planes_a[:].bitcast(I32), 0)
+        nc.vector.memset(planes_b[:].bitcast(I32), 0)
+        bias_row = keep.tile([P, H0 + H1], BF16)
+        nc.vector.memset(bias_row[:], 0.0)
+        c_bf16 = keep.tile([P, H1], BF16)
+        nc.vector.memset(c_bf16[:], 0.0)
+        ones = keep.tile([P, P], BF16)
+        nc.vector.memset(ones[:], 1.0)
+        identity = keep.tile([P, P], F32)
+        make_identity(nc, identity[:])
+
+        nc.scalar.dma_start(out=bias_row[0:1, 0:H0], in_=b1.rearrange("(o n) -> o n", o=1))
+        nc.scalar.dma_start(out=bias_row[0:1, H0 : H0 + H1], in_=b2.rearrange("(o n) -> o n", o=1))
+        nc.scalar.dma_start(out=c_bf16[0:CENTROIDS, :], in_=clusters)
+        table_in = keep.tile([P, 1], F32)
+        table_out = keep.tile([P, 1], F32)
+        nc.vector.memset(table_in[:], 0.0)
+        nc.scalar.activation(out=table_out[:], in_=table_in[:], func=ACT.Silu)
+
+        x_sb = []
+
+        def load_x(i):
+            x_tile = x_pool.tile([P, D_IN], BF16)
+            nc.sync.dma_start(out=x_tile[:], in_=x_tiles_dram[i])
+            x_sb.append(x_tile)
+
+        for i in group(0):
+            load_x(i)
+        for quadrant in range(4):
+            rows = slice(4 * quadrant, 4 * quadrant + 4)
+            first = 32 * quadrant
+            nc.sync.dma_start(
+                out=planes_a[first : first + 16, :].bitcast(I32), in_=W1_scales[0:4, rows, :].bitcast(I32)
+            )
+        for quadrant in range(4):
+            rows = slice(4 * quadrant, 4 * quadrant + 4)
+            first = 32 * quadrant
+            nc.sync.dma_start(
+                out=planes_b[first : first + 8, :].bitcast(I32), in_=W1_scales[4:6, rows, :].bitcast(I32)
+            )
+            nc.sync.dma_start(
+                out=planes_b[first + 8 : first + 16, 0:H1].bitcast(I32), in_=W2_scales[:, rows, :].bitcast(I32)
+            )
+        w1_sb = []
+        for g in range(PASSES_1):
+            w1_tile = w1_pool.tile([P, H0], U32, align_bytes=64)
+            nc.sync.dma_start(
+                out=w1_tile[:].bitcast(I32), in_=W1_words[g].rearrange("p n t -> p (n t)").bitcast(I32)
+            )
+            w1_sb.append(w1_tile)
+        w2_sb = keep.tile([P, PASSES_2, H1], U32, align_bytes=64)
+        for g in range(PASSES_2):
+            nc.sync.dma_start(
+                out=w2_sb[:, g, :].bitcast(I32), in_=W2_words[g].rearrange("p n t -> p (n t)").bitcast(I32)
+            )
+        for i in range(FIRST_GROUP, TILES):
+            load_x(i)
+
+        def w1_plane(g, cols):
+            tile_of_planes = planes_a if g < 4 else planes_b
+            return tile_of_planes[4 * (g % 4) : P, cols]
+
+        def w2_plane(g):
+            return planes_b[8 + 4 * g : P, 0:H1]
+
+        b1_planes = keep.tile([P, PASSES_2, PACK, P], F32)
+        b2_all = keep.tile([P, H1], F32)
+        c_f32 = keep.tile([P, H1], F32)
+        c_squares = keep.tile([P, H1], F32)
+        c_norm = keep.tile([P, 1], F32)
+        ct_minus2 = keep.tile([P, Z_HALVES, CENTROIDS_PAD], F32)
+        c_norm_plus1 = keep.tile([P, CENTROIDS_PAD], F32)
+        z_sb = keep.tile([P, TILES, H1], F32)
+        z_norm = keep.tile([P, TILES], F32)
+        d2_plus1 = keep.tile([P, TILES, CENTROIDS], F32)
+        t_sb = keep.tile([P, TILES, CENTROIDS], F32)
+        t_sum = keep.tile([P, TILES], F32)
+        t_scale = keep.tile([P, TILES], F32)
+        q_sb = keep.tile([P, TILES, CENTROIDS], F32)
+
+        x_codes, x_scales, sums, pre, h_codes, h_scales, z_sums, zt_sb, dots = {}, {}, {}, {}, {}, {}, {}, {}, {}
+
+        def transpose_x(i):
+            x_words = x_sb[i][:].bitcast(F32)
+            codes = work.tile([P, PASSES_1 * P], U32, align_bytes=64)
+            scales = work.tile([P, PASSES_1 * P], U8, align_bytes=64)
+            x_codes[i], x_scales[i] = codes, scales
+            for pair in range(PASSES_1 // 2):
+                xt = ps_x.tile([P, 2, 2, P], F32, tag="xt")
+                for s in range(2):
+                    first_word = (K_PASS // 2) * (2 * pair + s)
+                    for u in range(2):
+                        nc.tensor.transpose(
+                            xt[:, s, u, :], x_words[:, first_word + u : first_word + K_PASS // 2 : 2], identity[:]
+                        )
+                grouped = work.tile([P, 2, P, PACK], BF16, align_bytes=64)
+                nc.scalar.copy(out=grouped[:].bitcast(F32), in_=xt[:].rearrange("p s u n -> p s n u"))
+                cols = slice(2 * P * pair, 2 * P * (pair + 1))
+                nc.vector.quantize_mx(
+                    out=codes[:, cols].bitcast(FP8X4),
+                    scales=scales[:, cols],
+                    in_=grouped[:].rearrange("p s n t -> p (s n t)"),
+                )
+
+        def constants():
+            for half in range(PASSES_2):
+                spread = ps_h.tile([P, BANK], F32, tag="bank")
+                nc.tensor.matmul(
+                    out=spread[:], lhsT=ones[:], rhs=bias_row[:, BANK * half : BANK * (half + 1)], start=True, stop=True
+                )
+                nc.vector.tensor_copy(
+                    out=b1_planes[:, half, :, :], in_=spread[:].rearrange("n (p t) -> n t p", t=PACK)
+                )
+            spread = ps_h.tile([P, BANK], F32, tag="bank")
+            nc.tensor.matmul(out=spread[:, 0:H1], lhsT=ones[:], rhs=bias_row[:, H0 : H0 + H1], start=True, stop=True)
+            nc.vector.tensor_copy(out=b2_all[:], in_=spread[:, 0:H1])
+
+            nc.vector.tensor_copy(out=c_f32[:], in_=c_bf16[:])
+            nc.scalar.activation(out=c_squares[:], in_=c_f32[:], func=ACT.Square, accum_out=c_norm[:])
+            ct = ps_h.tile([P, Z_HALVES, P], F32, tag="bank")
+            for half in range(Z_HALVES):
+                nc.tensor.transpose(ct[:, half, :], c_f32[:, P * half : P * (half + 1)], identity[:])
+            nc.vector.tensor_scalar_mul(out=ct_minus2[:], in0=ct[:, :, 0:CENTROIDS_PAD], scalar1=-2.0)
+            norms = ps_h.tile([P, BANK], F32, tag="bank")
+            nc.tensor.matmul(
+                out=norms[:, 0:CENTROIDS_PAD],
+                lhsT=c_norm[:, 0:1].to_broadcast([P, P]),
+                rhs=identity[:, 0:CENTROIDS_PAD],
+                start=True,
+                stop=True,
+            )
+            nc.vector.tensor_scalar_add(out=c_norm_plus1[:], in0=norms[:, 0:CENTROIDS_PAD], scalar1=1.0)
+
+        def layer1(tiles):
+            for i in tiles:
+                for half in range(PASSES_2):
+                    bank = ps_h.tile([P, BANK], F32, tag="bank")
+                    sums[(i, half)] = bank
+            for g in range(PASSES_1):
+                for i in tiles:
+                    for half in range(PASSES_2):
+                        cols = slice(BANK * half, BANK * (half + 1))
+                        nc.tensor.matmul_mx(
+                            out=sums[(i, half)][:],
+                            lhsT=x_codes[i][:, P * g : P * (g + 1)].bitcast(FP8X4),
+                            lhsT_scale=x_scales[i][:, P * g : P * (g + 1)],
+                            rhs=w1_sb[g][:, cols].bitcast(FP8X4),
+                            rhs_scale=w1_plane(g, cols),
+                            start=(g == 0),
+                            stop=(g == PASSES_1 - 1),
+                        )
+
+        def add_b1(i):
+            for half in range(PASSES_2):
+                planes = work.tile([P, PACK, P], F32)
+                nc.vector.tensor_tensor(
+                    out=planes[:],
+                    in0=sums[(i, half)][:].rearrange("n (p t) -> n t p", t=PACK),
+                    in1=b1_planes[:, half, :, :],
+                    op=ALU.add,
+                )
+                pre[(i, half)] = planes
+
+        def transpose_h(i):
+            grouped_h = work.tile([P, PASSES_2, P, PACK], BF16, align_bytes=64)
+            for half in range(PASSES_2):
+                ht = ps_h.tile([P, PACK, P], F32, tag="bank")
+                for t in range(PACK):
+                    nc.tensor.transpose(ht[:, t, :], pre[(i, half)][:, t, :], identity[:])
+                nc.scalar.activation(
+                    out=grouped_h[:, half, :, :], in_=ht[:].rearrange("p t n -> p n t"), func=ACT.Silu
+                )
+            codes_h = work.tile([P, PASSES_2 * P], U32, align_bytes=64)
+            scales_h = work.tile([P, PASSES_2 * P], U8, align_bytes=64)
+            nc.vector.quantize_mx(
+                out=codes_h[:].bitcast(FP8X4),
+                scales=scales_h[:],
+                in_=grouped_h[:].rearrange("p g n t -> p (g n t)"),
+            )
+            h_codes[i], h_scales[i] = codes_h, scales_h
+
+        def layer2(tiles):
+            if not tiles:
+                return
+            bank_z = ps_z.tile([P, FIRST_GROUP, H1], F32)
+            for slot, i in enumerate(tiles):
+                z_sums[i] = bank_z[:, slot, :]
+                for g in range(PASSES_2):
+                    nc.tensor.matmul_mx(
+                        out=z_sums[i],
+                        lhsT=h_codes[i][:, P * g : P * (g + 1)].bitcast(FP8X4),
+                        lhsT_scale=h_scales[i][:, P * g : P * (g + 1)],
+                        rhs=w2_sb[:, g, :].bitcast(FP8X4),
+                        rhs_scale=w2_plane(g),
+                        start=(g == 0),
+                        stop=(g == PASSES_2 - 1),
+                    )
+
+        def finish_z(i):
+            nc.vector.tensor_tensor(out=z_sb[:, i, :], in0=z_sums[i], in1=b2_all[:], op=ALU.add)
+            nc.sync.dma_start(out=z_tiles_dram[i], in_=z_sb[:, i, :])
+
+        def transpose_z(i):
+            zt = ps_x.tile([P, Z_HALVES, P], F32, tag="xt")
+            for half in range(Z_HALVES):
+                nc.tensor.transpose(zt[:, half, :], z_sb[:, i, P * half : P * (half + 1)], identity[:])
+            zt_copy = work.tile([P, Z_HALVES, P], F32)
+            nc.scalar.copy(out=zt_copy[:], in_=zt[:])
+            zt_sb[i] = zt_copy
+            z_squares = work.tile([P, H1], F32)
+            nc.scalar.activation(
+                out=z_squares[:], in_=z_sb[:, i, :], func=ACT.Square, accum_out=z_norm[:, i : i + 1]
+            )
+
+        def centroid_products(i):
+            dot = ps_h.tile([P, BANK], F32, tag="bank")
+            for half in range(Z_HALVES):
+                nc.tensor.matmul(
+                    out=dot[:, 0:CENTROIDS_PAD],
+                    lhsT=zt_sb[i][:, half, :],
+                    rhs=ct_minus2[:, half, :],
+                    start=(half == 0),
+                    stop=(half == Z_HALVES - 1),
+                )
+            dots[i] = dot
+
+        def soft_assignment(i):
+            nc.vector.scalar_tensor_tensor(
+                out=d2_plus1[:, i, :],
+                in0=dots[i][:, 0:CENTROIDS],
+                scalar=z_norm[:, i : i + 1],
+                in1=c_norm_plus1[:, 0:CENTROIDS],
+                op0=ALU.add,
+                op1=ALU.add,
+            )
+            nc.vector.reciprocal(out=t_sb[:, i, :], in_=d2_plus1[:, i, :])
+            nc.vector.reduce_sum(out=t_sum[:, i : i + 1], in_=t_sb[:, i, :], axis=AXIS.X)
+            nc.vector.reciprocal(out=t_scale[:, i : i + 1], in_=t_sum[:, i : i + 1])
+            nc.vector.tensor_scalar_mul(out=q_sb[:, i, :], in0=t_sb[:, i, :], scalar1=t_scale[:, i : i + 1])
+
+        for i in group(0):
+            transpose_x(i)
+        constants()
+        for a in range(len(groups) + 2):
+            layer1(group(a))
+            layer2(group(a - 1))
+            for i in group(a):
+                add_b1(i)
+            for i in group(a - 1):
+                finish_z(i)
+            for i in group(a - 2):
+                centroid_products(i)
+            for i in group(a + 1):
+                transpose_x(i)
+            for i in group(a - 1):
+                transpose_z(i)
+            for i in group(a):
+                transpose_h(i)
+            for i in group(a - 2):
+                soft_assignment(i)
+        nc.sync.dma_start(
+            out=out_1.rearrange("(p i) k -> p (i k)", i=TILES), in_=q_sb[:].rearrange("p i k -> p (i k)")
+        )

@@ -133,7 +133,7 @@ def tile_lintrans_pa_kernel(
         t_scale = keep.tile([P, TILES], F32)
         q_sb = keep.tile([P, TILES, CENTROIDS], F32)
 
-        x_codes, x_scales, sums, pre, h_codes, h_scales, z_sums, zt_sb, dots = {}, {}, {}, {}, {}, {}, {}, {}, {}
+        x_codes, x_scales, sums, pre, h_codes, h_scales, z_sums, zt_sb = {}, {}, {}, {}, {}, {}, {}, {}
 
         def transpose_x(i):
             x_words = x_sb[i][:].bitcast(F32)
@@ -277,17 +277,16 @@ def tile_lintrans_pa_kernel(
                     start=(half == 0),
                     stop=(half == Z_HALVES - 1),
                 )
-            dots[i] = dot
-
-        def soft_assignment(i):
             nc.vector.scalar_tensor_tensor(
                 out=d2_plus1[:, i, :],
-                in0=dots[i][:, 0:CENTROIDS],
+                in0=dot[:, 0:CENTROIDS],
                 scalar=z_norm[:, i : i + 1],
                 in1=c_norm_plus1[:, 0:CENTROIDS],
                 op0=ALU.add,
                 op1=ALU.add,
             )
+
+        def soft_assignment(i):
             nc.vector.reciprocal(out=t_sb[:, i, :], in_=d2_plus1[:, i, :])
             nc.vector.reduce_sum(out=t_sum[:, i : i + 1], in_=t_sb[:, i, :], axis=AXIS.X)
             nc.vector.reciprocal(out=t_scale[:, i : i + 1], in_=t_sum[:, i : i + 1])
@@ -307,10 +306,10 @@ def tile_lintrans_pa_kernel(
                 centroid_products(i)
             for i in group(a + 1):
                 transpose_x(i)
-            for i in group(a - 1):
-                transpose_z(i)
             for i in group(a):
                 transpose_h(i)
+            for i in group(a - 1):
+                transpose_z(i)
             for i in group(a - 2):
                 soft_assignment(i)
         nc.sync.dma_start(

@@ -16,15 +16,19 @@ AXIS = mybir.AxisListType
 P = 128
 PACK = 4
 K_PASS = P * PACK
-BANK = 512
+WORDS = K_PASS // 2
 
 TOKENS, D_IN, H0, H1, CENTROIDS = 1024, 3072, 1024, 256, 20
 TILES = TOKENS // P
+PAIR = 2
+GROUPS = TILES // PAIR
+GT = PAIR * P
 PASSES_1 = D_IN // K_PASS
 PASSES_2 = H0 // K_PASS
+HALF = H0 // PASSES_2
 Z_HALVES = H1 // P
 CENTROIDS_PAD = 32
-FIRST_GROUP = 2
+CHUNK = 2
 
 FLOPS = 2 * TOKENS * D_IN * H0 + 2 * TOKENS * H0 * H1
 
@@ -33,54 +37,64 @@ def tile_lintrans_pa_kernel(
     tc, x, W1_words, W1_scales, b1, W2_words, W2_scales, b2, clusters, out_0, out_1
 ):
     nc = tc.nc
-    groups = [list(range(FIRST_GROUP))] + [[i] for i in range(FIRST_GROUP, TILES)]
-
-    def group(a):
-        return groups[a] if 0 <= a < len(groups) else []
-
-    x_tiles_dram = x.rearrange("(p i) k -> i p k", i=TILES)
-    z_tiles_dram = out_0.rearrange("(p i) j -> i p j", i=TILES)
+    x_dram = x.rearrange("(p i) k -> p i k", i=TILES)
+    q_dram = out_1.rearrange("(p i) k -> p (i k)", i=TILES)
+    z_dram = out_0.rearrange("(p i) j -> p i j", i=TILES)
 
     with ExitStack() as ctx:
         keep = ctx.enter_context(tc.tile_pool(name="keep", bufs=1))
-        x_pool = ctx.enter_context(tc.tile_pool(name="x_pool", bufs=TILES))
-        w1_pool = ctx.enter_context(tc.tile_pool(name="w1_pool", bufs=PASSES_1))
+        x_pool = ctx.enter_context(tc.tile_pool(name="x_pool", bufs=GROUPS * PASSES_1 // CHUNK))
+        w1_pool = ctx.enter_context(tc.tile_pool(name="w1_pool", bufs=PASSES_1 * PASSES_2))
         work = ctx.enter_context(tc.tile_pool(name="work", bufs=4))
+        grouped_pool = ctx.enter_context(tc.tile_pool(name="grouped_pool", bufs=8))
         ps_x = ctx.enter_context(tc.psum_pool(name="ps_x", bufs=3))
-        ps_h = ctx.enter_context(tc.psum_pool(name="ps_h", bufs=4))
-        ps_z = ctx.enter_context(tc.psum_pool(name="ps_z", bufs=1))
+        ps_h = ctx.enter_context(tc.psum_pool(name="ps_h", bufs=5))
         ctx.enter_context(tc.manual_schedule())
 
+        table_in = keep.tile([P, 1], F32)
+        table_out = keep.tile([P, 1], F32)
+        nc.vector.memset(table_in[:], 0.0)
         planes_a = keep.tile([P, H0], U8, align_bytes=64)
         planes_b = keep.tile([P, H0], U8, align_bytes=64)
         nc.vector.memset(planes_a[:].bitcast(I32), 0)
         nc.vector.memset(planes_b[:].bitcast(I32), 0)
-        bias_row = keep.tile([P, H0 + H1], BF16)
-        nc.vector.memset(bias_row[:], 0.0)
-        c_bf16 = keep.tile([P, H1], BF16)
-        nc.vector.memset(c_bf16[:], 0.0)
-        ones = keep.tile([P, P], BF16)
-        nc.vector.memset(ones[:], 1.0)
         identity = keep.tile([P, P], F32)
         make_identity(nc, identity[:])
+        c_bf16 = keep.tile([P, H1], BF16)
+        nc.gpsimd.memset(c_bf16[:], 0.0)
+        b2_row = keep.tile([P, H1], BF16)
+        nc.gpsimd.memset(b2_row[:], 0.0)
+        ones = keep.tile([P, P], BF16)
+        nc.gpsimd.memset(ones[:], 1.0)
 
-        nc.scalar.dma_start(out=bias_row[0:1, 0:H0], in_=b1.rearrange("(o n) -> o n", o=1))
-        nc.scalar.dma_start(out=bias_row[0:1, H0 : H0 + H1], in_=b2.rearrange("(o n) -> o n", o=1))
-        nc.scalar.dma_start(out=c_bf16[0:CENTROIDS, :], in_=clusters)
-        table_in = keep.tile([P, 1], F32)
-        table_out = keep.tile([P, 1], F32)
-        nc.vector.memset(table_in[:], 0.0)
+        b1_cols_bf16 = keep.tile([P, PASSES_2, PACK], BF16)
+        nc.scalar.dma_start(out=b1_cols_bf16[:], in_=b1.rearrange("(c p t) -> p c t", c=PASSES_2, t=PACK))
         nc.scalar.activation(out=table_out[:], in_=table_in[:], func=ACT.Silu)
+        nc.gpsimd.dma_start(out=c_bf16[0:CENTROIDS, :], in_=clusters)
+        nc.gpsimd.dma_start(out=b2_row[0:1, :], in_=b2.rearrange("(o n) -> o n", o=1))
 
-        x_sb = []
+        x_sb = {}
 
-        def load_x(i):
-            x_tile = x_pool.tile([P, D_IN], BF16)
-            nc.sync.dma_start(out=x_tile[:], in_=x_tiles_dram[i])
-            x_sb.append(x_tile)
+        def load_x(a):
+            for c in range(PASSES_1 // CHUNK):
+                x_tile = x_pool.tile([P, PAIR, CHUNK * K_PASS], BF16)
+                cols = slice(CHUNK * K_PASS * c, CHUNK * K_PASS * (c + 1))
+                nc.sync.dma_start(out=x_tile[:], in_=x_dram[:, PAIR * a : PAIR * (a + 1), cols])
+                x_sb[(a, c)] = x_tile
 
-        for i in group(0):
-            load_x(i)
+        w1_raw = {}
+
+        def load_w1(half):
+            for g in range(PASSES_1):
+                raw = w1_pool.tile([P, HALF], U32, align_bytes=64)
+                words = W1_words[g].rearrange("p n t -> p (n t)")
+                nc.sync.dma_start(
+                    out=raw[:].bitcast(I32),
+                    in_=words[:, PACK * HALF * half : PACK * HALF * (half + 1)].bitcast(I32),
+                )
+                w1_raw[(half, g)] = raw
+
+        load_x(0)
         for quadrant in range(4):
             rows = slice(4 * quadrant, 4 * quadrant + 4)
             first = 32 * quadrant
@@ -96,34 +110,25 @@ def tile_lintrans_pa_kernel(
             nc.sync.dma_start(
                 out=planes_b[first + 8 : first + 16, 0:H1].bitcast(I32), in_=W2_scales[:, rows, :].bitcast(I32)
             )
-        w1_sb = []
-        for g in range(PASSES_1):
-            w1_tile = w1_pool.tile([P, H0], U32, align_bytes=64)
-            nc.sync.dma_start(
-                out=w1_tile[:].bitcast(I32), in_=W1_words[g].rearrange("p n t -> p (n t)").bitcast(I32)
-            )
-            w1_sb.append(w1_tile)
+        load_w1(0)
+        load_x(1)
+        load_w1(1)
         w2_sb = keep.tile([P, PASSES_2, H1], U32, align_bytes=64)
         for g in range(PASSES_2):
             nc.sync.dma_start(
                 out=w2_sb[:, g, :].bitcast(I32), in_=W2_words[g].rearrange("p n t -> p (n t)").bitcast(I32)
             )
-        for i in range(FIRST_GROUP, TILES):
-            load_x(i)
+        for a in range(2, GROUPS):
+            load_x(a)
 
-        def w1_plane(g, cols):
-            tile_of_planes = planes_a if g < 4 else planes_b
-            return tile_of_planes[4 * (g % 4) : P, cols]
-
-        def w2_plane(g):
-            return planes_b[8 + 4 * g : P, 0:H1]
-
-        b1_planes = keep.tile([P, PASSES_2, PACK, P], F32)
-        b2_all = keep.tile([P, H1], F32)
+        b1_cols = keep.tile([P, PASSES_2, PACK], F32)
+        planes_1 = keep.tile([P, 2, PASSES_2, PACK, P], U8, align_bytes=64)
+        b2_all = keep.tile([P, PAIR, H1], F32)
         c_f32 = keep.tile([P, H1], F32)
-        c_squares = keep.tile([P, H1], F32)
+        c_less = keep.tile([P, H1], F32)
+        c_prod = keep.tile([P, H1], F32)
         c_norm = keep.tile([P, 1], F32)
-        ct_minus2 = keep.tile([P, Z_HALVES, CENTROIDS_PAD], F32)
+        ct_minus2 = keep.tile([P, Z_HALVES, CENTROIDS_PAD], BF16)
         c_norm_plus1 = keep.tile([P, CENTROIDS_PAD], F32)
         z_sb = keep.tile([P, TILES, H1], F32)
         z_norm = keep.tile([P, TILES], F32)
@@ -133,50 +138,292 @@ def tile_lintrans_pa_kernel(
         t_scale = keep.tile([P, TILES], F32)
         q_sb = keep.tile([P, TILES, CENTROIDS], F32)
 
-        x_codes, x_scales, sums, pre, h_codes, h_scales, z_sums, zt_sb = {}, {}, {}, {}, {}, {}, {}, {}
+        x_codes, x_scales, w1, sums, h_raw, h_codes, h_scales = {}, {}, {}, {}, {}, {}, {}
+        z_bank, zt_bank, zt_hi, zt_lo, dots = {}, {}, {}, {}, {}
 
-        def transpose_x(i):
-            x_words = x_sb[i][:].bitcast(F32)
-            codes = work.tile([P, PASSES_1 * P], U32, align_bytes=64)
-            scales = work.tile([P, PASSES_1 * P], U8, align_bytes=64)
-            x_codes[i], x_scales[i] = codes, scales
-            for pair in range(PASSES_1 // 2):
-                xt = ps_x.tile([P, 2, 2, P], F32, tag="xt")
-                for s in range(2):
-                    first_word = (K_PASS // 2) * (2 * pair + s)
+        def transpose_x(a, passes):
+            grouped = {}
+            for g in passes:
+                xt = ps_x.tile([P, PAIR, 2, P], F32, tag="xt")
+                for i in range(PAIR):
+                    words = x_sb[(a, g // CHUNK)][:, i, :].bitcast(F32)
+                    first = WORDS * (g % CHUNK)
                     for u in range(2):
-                        nc.tensor.transpose(
-                            xt[:, s, u, :], x_words[:, first_word + u : first_word + K_PASS // 2 : 2], identity[:]
-                        )
-                grouped = work.tile([P, 2, P, PACK], BF16, align_bytes=64)
-                nc.scalar.copy(out=grouped[:].bitcast(F32), in_=xt[:].rearrange("p s u n -> p s n u"))
-                cols = slice(2 * P * pair, 2 * P * (pair + 1))
+                        nc.tensor.transpose(xt[:, i, u, :], words[:, first + u : first + WORDS : 2], identity[:])
+                out = grouped_pool.tile([P, PAIR, P, PACK], BF16, align_bytes=64)
+                nc.scalar.copy(out=out[:].bitcast(F32), in_=xt[:].rearrange("p i u n -> p i n u"))
+                grouped[g] = out
+            return grouped
+
+        def quantise_x(a, grouped):
+            if a not in x_codes:
+                codes = work.tile([P, PASSES_1, GT], U32, align_bytes=64)
+                scales = work.tile([P, PASSES_1, GT], U8, align_bytes=64)
+                x_codes[a], x_scales[a] = codes, scales
+            for g in grouped:
                 nc.vector.quantize_mx(
-                    out=codes[:, cols].bitcast(FP8X4),
-                    scales=scales[:, cols],
-                    in_=grouped[:].rearrange("p s n t -> p (s n t)"),
+                    out=x_codes[a][:, g, :].bitcast(FP8X4),
+                    scales=x_scales[a][:, g, :],
+                    in_=grouped[g][:].rearrange("p i n t -> p (i n t)"),
                 )
+
+        def permute_planes(half):
+            for s, planes in enumerate((planes_a, planes_b)):
+                nc.vector.tensor_copy(
+                    out=planes_1[:, s, half, :, :].rearrange("p t m -> p m t"),
+                    in_=planes[:, HALF * half : HALF * (half + 1)].rearrange("p (m t) -> p m t", t=PACK),
+                )
+
+        def permute_w1(half, passes):
+            for g in passes:
+                permuted = w1_pool.tile([P, PACK, P], U32, align_bytes=64)
+                nc.vector.tensor_copy(
+                    out=permuted[:].bitcast(I32).rearrange("p t m -> p m t"),
+                    in_=w1_raw[(half, g)][:].bitcast(I32).rearrange("p (m t) -> p m t", t=PACK),
+                )
+                w1[(half, g)] = permuted
+
+        def layer1(a, half, by_pass):
+            def one(t, g):
+                nc.tensor.matmul_mx(
+                    out=sums[(a, half, t)],
+                    lhsT=w1[(half, g)][:, t, :].bitcast(FP8X4),
+                    lhsT_scale=planes_1[4 * (g % 4) : P, g // 4, half, t, :],
+                    rhs=x_codes[a][:, g, :].bitcast(FP8X4),
+                    rhs_scale=x_scales[a][:, g, :],
+                    start=(g == 0),
+                    stop=(g == PASSES_1 - 1),
+                )
+
+            if by_pass:
+                for t in range(PACK):
+                    bank = ps_h.tile([P, 2, GT], F32, tag="bank")
+                    sums[(a, half, t)] = bank[:, 0, :]
+                for g in range(PASSES_1):
+                    for t in range(PACK):
+                        one(t, g)
+                return
+            for t in range(PACK):
+                if t % 2 == 0:
+                    bank = ps_h.tile([P, 2, GT], F32, tag="bank")
+                sums[(a, half, t)] = bank[:, t % 2, :]
+                for g in range(PASSES_1):
+                    one(t, g)
+
+        def layer1_tile(a, half, i):
+            for t in range(PACK):
+                if t in (0, PACK - 1):
+                    bank = ps_h.tile([P, PACK - 1, P], F32, tag="bank")
+                sums[(a, half, t, i)] = bank[:, t % (PACK - 1), :]
+                for g in range(PASSES_1):
+                    nc.tensor.matmul_mx(
+                        out=sums[(a, half, t, i)],
+                        lhsT=w1[(half, g)][:, t, :].bitcast(FP8X4),
+                        lhsT_scale=planes_1[4 * (g % 4) : P, g // 4, half, t, :],
+                        rhs=x_codes[a][:, g, P * i : P * (i + 1)].bitcast(FP8X4),
+                        rhs_scale=x_scales[a][:, g, P * i : P * (i + 1)],
+                        start=(g == 0),
+                        stop=(g == PASSES_1 - 1),
+                    )
+
+        def silu_tile(a, half, i):
+            raw = work.tile([P, PACK, P], BF16, align_bytes=64, tag="raw_tile")
+            for t in range(PACK):
+                nc.scalar.activation(
+                    out=raw[:, t, :], in_=sums[(a, half, t, i)], func=ACT.Silu, bias=b1_cols[:, half, t : t + 1]
+                )
+            h_raw[(a, half, i)] = raw
+
+        def interleave_tile(a, half, i):
+            grouped = work.tile([P, P, PACK], BF16, align_bytes=64, tag="grouped_tile")
+            nc.vector.tensor_copy(out=grouped[:], in_=h_raw[(a, half, i)][:].rearrange("p t n -> p n t"))
+            h_raw[(a, half, i)] = grouped
+
+        def quantise_tile(a, half, i):
+            cols = slice(P * i, P * (i + 1))
+            nc.vector.quantize_mx(
+                out=h_codes[a][:, half, cols].bitcast(FP8X4),
+                scales=h_scales[a][:, half, cols],
+                in_=h_raw[(a, half, i)][:].rearrange("p n t -> p (n t)"),
+            )
+
+        def layer2_tile(a, i):
+            cols = slice(P * i, P * (i + 1))
+            z_bank[(a, i)] = ps_x.tile([P, H1], F32, tag="xt", name="z_tile")
+            zt_bank[(a, i)] = ps_x.tile([P, Z_HALVES, P], F32, tag="xt", name="zt_tile")
+            for g in range(PASSES_2):
+                nc.tensor.matmul_mx(
+                    out=z_bank[(a, i)][:],
+                    lhsT=h_codes[a][:, g, cols].bitcast(FP8X4),
+                    lhsT_scale=h_scales[a][:, g, cols],
+                    rhs=w2_sb[:, g, :].bitcast(FP8X4),
+                    rhs_scale=planes_b[8 + 4 * g : P, 0:H1],
+                    start=(g == 0),
+                    stop=(g == PASSES_2 - 1),
+                )
+            for j in range(Z_HALVES):
+                rows = slice(P * j, P * (j + 1))
+                for g in range(PASSES_2):
+                    nc.tensor.matmul_mx(
+                        out=zt_bank[(a, i)][:, j, :],
+                        lhsT=w2_sb[:, g, rows].bitcast(FP8X4),
+                        lhsT_scale=planes_b[8 + 4 * g : P, rows],
+                        rhs=h_codes[a][:, g, cols].bitcast(FP8X4),
+                        rhs_scale=h_scales[a][:, g, cols],
+                        start=(g == 0),
+                        stop=(g == PASSES_2 - 1),
+                    )
+
+        def add_b2_tile(a, i):
+            tile = PAIR * a + i
+            nc.vector.tensor_tensor(out=z_sb[:, tile, :], in0=z_bank[(a, i)][:], in1=b2_all[:, 0, :], op=ALU.add)
+            nc.sync.dma_start(out=z_dram[:, tile, :], in_=z_sb[:, tile, :])
+
+        def hi_tile(a, i):
+            hi = work.tile([P, Z_HALVES, P], BF16, tag="hi_tile")
+            nc.scalar.copy(out=hi[:], in_=zt_bank[(a, i)][:])
+            zt_hi[(a, i)] = hi
+
+        def lo_tile(a, i):
+            lo = work.tile([P, Z_HALVES, P], BF16, tag="lo_tile")
+            nc.vector.tensor_tensor(out=lo[:], in0=zt_bank[(a, i)][:], in1=zt_hi[(a, i)][:], op=ALU.subtract)
+            zt_lo[(a, i)] = lo
+
+        def square_tile(a, i):
+            tile = PAIR * a + i
+            z_squares = work.tile([P, H1], F32)
+            nc.scalar.activation(
+                out=z_squares[:], in_=z_sb[:, tile, :], func=ACT.Square, accum_out=z_norm[:, tile : tile + 1]
+            )
+
+        def silu(a, half):
+            raw = work.tile([P, PACK, GT], BF16, align_bytes=64)
+            for t in range(PACK):
+                nc.scalar.activation(
+                    out=raw[:, t, :], in_=sums[(a, half, t)], func=ACT.Silu, bias=b1_cols[:, half, t : t + 1]
+                )
+            h_raw[(a, half)] = raw
+
+        def quantise_h(a, half):
+            if a not in h_codes:
+                codes = work.tile([P, PASSES_2, GT], U32, align_bytes=64, tag="h_codes")
+                scales = work.tile([P, PASSES_2, GT], U8, align_bytes=64, tag="h_scales")
+                h_codes[a], h_scales[a] = codes, scales
+            grouped = work.tile([P, PAIR, P, PACK], BF16, align_bytes=64, tag="grouped_h")
+            for i in range(PAIR):
+                nc.vector.tensor_copy(
+                    out=grouped[:, i, :, :],
+                    in_=h_raw[(a, half)][:, :, P * i : P * (i + 1)].rearrange("p t n -> p n t"),
+                )
+            for i in range(PAIR):
+                nc.vector.quantize_mx(
+                    out=h_codes[a][:, half, P * i : P * (i + 1)].bitcast(FP8X4),
+                    scales=h_scales[a][:, half, P * i : P * (i + 1)],
+                    in_=grouped[:, i, :, :].rearrange("p n t -> p (n t)"),
+                )
+
+        def layer2(a):
+            z_bank[a] = ps_h.tile([P, PAIR, H1], F32, tag="bank", name="z_sums")
+            zt_bank[a] = ps_h.tile([P, Z_HALVES, GT], F32, tag="bank", name="zt_sums")
+            for i in range(PAIR):
+                for g in range(PASSES_2):
+                    nc.tensor.matmul_mx(
+                        out=z_bank[a][:, i, :],
+                        lhsT=h_codes[a][:, g, P * i : P * (i + 1)].bitcast(FP8X4),
+                        lhsT_scale=h_scales[a][:, g, P * i : P * (i + 1)],
+                        rhs=w2_sb[:, g, :].bitcast(FP8X4),
+                        rhs_scale=planes_b[8 + 4 * g : P, 0:H1],
+                        start=(g == 0),
+                        stop=(g == PASSES_2 - 1),
+                    )
+            for j in range(Z_HALVES):
+                cols = slice(P * j, P * (j + 1))
+                for g in range(PASSES_2):
+                    nc.tensor.matmul_mx(
+                        out=zt_bank[a][:, j, :],
+                        lhsT=w2_sb[:, g, cols].bitcast(FP8X4),
+                        lhsT_scale=planes_b[8 + 4 * g : P, cols],
+                        rhs=h_codes[a][:, g, :].bitcast(FP8X4),
+                        rhs_scale=h_scales[a][:, g, :],
+                        start=(g == 0),
+                        stop=(g == PASSES_2 - 1),
+                    )
+
+        def finish_z(a):
+            tiles = slice(PAIR * a, PAIR * (a + 1))
+            nc.vector.tensor_tensor(out=z_sb[:, tiles, :], in0=z_bank[a][:], in1=b2_all[:], op=ALU.add)
+            nc.sync.dma_start(out=z_dram[:, tiles, :], in_=z_sb[:, tiles, :])
+            hi = work.tile([P, Z_HALVES, GT], BF16, tag="zt_hi")
+            nc.scalar.copy(out=hi[:], in_=zt_bank[a][:])
+            lo = work.tile([P, Z_HALVES, GT], BF16, tag="zt_lo")
+            nc.vector.tensor_tensor(out=lo[:], in0=zt_bank[a][:], in1=hi[:], op=ALU.subtract)
+            zt_hi[a], zt_lo[a] = hi, lo
+            for i in range(PAIR * a, PAIR * (a + 1)):
+                z_squares = work.tile([P, H1], F32)
+                nc.scalar.activation(
+                    out=z_squares[:], in_=z_sb[:, i, :], func=ACT.Square, accum_out=z_norm[:, i : i + 1]
+                )
+
+        def products(out, hi, lo, cols):
+            parts = [(part, j) for part in (hi, lo) for j in range(Z_HALVES)]
+            for n, (part, j) in enumerate(parts):
+                nc.tensor.matmul(
+                    out=out,
+                    lhsT=part[:, j, cols],
+                    rhs=ct_minus2[:, j, :],
+                    start=(n == 0),
+                    stop=(n == len(parts) - 1),
+                )
+
+        def distances(a, i, dot):
+            tile = PAIR * a + i
+            nc.vector.scalar_tensor_tensor(
+                out=d2_plus1[:, tile, :],
+                in0=dot[:, 0:CENTROIDS],
+                scalar=z_norm[:, tile : tile + 1],
+                in1=c_norm_plus1[:, 0:CENTROIDS],
+                op0=ALU.add,
+                op1=ALU.add,
+            )
+
+        def normalise(a):
+            tiles = slice(PAIR * a, PAIR * (a + 1))
+            nc.vector.reciprocal(out=t_sb[:, tiles, :], in_=d2_plus1[:, tiles, :])
+            nc.vector.reduce_sum(out=t_sum[:, tiles], in_=t_sb[:, tiles, :], axis=AXIS.X)
+            nc.vector.reciprocal(out=t_scale[:, tiles], in_=t_sum[:, tiles])
+            for tile in range(PAIR * a, PAIR * (a + 1)):
+                nc.vector.tensor_scalar_mul(
+                    out=q_sb[:, tile, :], in0=t_sb[:, tile, :], scalar1=t_scale[:, tile : tile + 1]
+                )
+
+        def group_products(a):
+            bank = ps_h.tile([P, PAIR, CENTROIDS_PAD], F32, tag="bank", name="dots")
+            for i in range(PAIR):
+                products(bank[:, i, :], zt_hi[a], zt_lo[a], slice(P * i, P * (i + 1)))
+            dots[a] = bank
+
+        def soft_assignment(a):
+            for i in range(PAIR):
+                distances(a, i, dots[a][:, i, :])
+            normalise(a)
 
         def constants():
-            for half in range(PASSES_2):
-                spread = ps_h.tile([P, BANK], F32, tag="bank")
-                nc.tensor.matmul(
-                    out=spread[:], lhsT=ones[:], rhs=bias_row[:, BANK * half : BANK * (half + 1)], start=True, stop=True
-                )
-                nc.vector.tensor_copy(
-                    out=b1_planes[:, half, :, :], in_=spread[:].rearrange("n (p t) -> n t p", t=PACK)
-                )
-            spread = ps_h.tile([P, BANK], F32, tag="bank")
-            nc.tensor.matmul(out=spread[:, 0:H1], lhsT=ones[:], rhs=bias_row[:, H0 : H0 + H1], start=True, stop=True)
-            nc.vector.tensor_copy(out=b2_all[:], in_=spread[:, 0:H1])
-
-            nc.vector.tensor_copy(out=c_f32[:], in_=c_bf16[:])
-            nc.scalar.activation(out=c_squares[:], in_=c_f32[:], func=ACT.Square, accum_out=c_norm[:])
+            spread = ps_h.tile([P, PAIR, H1], F32, tag="bank")
+            for i in range(PAIR):
+                nc.tensor.matmul(out=spread[:, i, :], lhsT=ones[:], rhs=b2_row[:], start=True, stop=True)
             ct = ps_h.tile([P, Z_HALVES, P], F32, tag="bank")
-            for half in range(Z_HALVES):
-                nc.tensor.transpose(ct[:, half, :], c_f32[:, P * half : P * (half + 1)], identity[:])
+            for j in range(Z_HALVES):
+                nc.tensor.transpose(ct[:, j, :], c_f32[:, P * j : P * (j + 1)], identity[:])
+            nc.vector.tensor_copy(out=b2_all[:], in_=spread[:])
             nc.vector.tensor_scalar_mul(out=ct_minus2[:], in0=ct[:, :, 0:CENTROIDS_PAD], scalar1=-2.0)
-            norms = ps_h.tile([P, BANK], F32, tag="bank")
+            nc.vector.scalar_tensor_tensor(
+                out=c_less[:], in0=b2_all[:, 0, :], scalar=-2.0, in1=c_f32[:], op0=ALU.mult, op1=ALU.add
+            )
+            nc.vector.tensor_tensor(out=c_prod[:], in0=c_less[:], in1=c_f32[:], op=ALU.mult)
+            nc.vector.reduce_sum(out=c_norm[:], in_=c_prod[:], axis=AXIS.X)
+
+        def spread_c_norm():
+            norms = ps_h.tile([P, P], F32, tag="bank")
             nc.tensor.matmul(
                 out=norms[:, 0:CENTROIDS_PAD],
                 lhsT=c_norm[:, 0:1].to_broadcast([P, P]),
@@ -186,132 +433,103 @@ def tile_lintrans_pa_kernel(
             )
             nc.vector.tensor_scalar_add(out=c_norm_plus1[:], in0=norms[:, 0:CENTROIDS_PAD], scalar1=1.0)
 
-        def layer1(tiles):
-            for i in tiles:
-                for half in range(PASSES_2):
-                    bank = ps_h.tile([P, BANK], F32, tag="bank")
-                    sums[(i, half)] = bank
-            for g in range(PASSES_1):
-                for i in tiles:
-                    for half in range(PASSES_2):
-                        cols = slice(BANK * half, BANK * (half + 1))
-                        nc.tensor.matmul_mx(
-                            out=sums[(i, half)][:],
-                            lhsT=x_codes[i][:, P * g : P * (g + 1)].bitcast(FP8X4),
-                            lhsT_scale=x_scales[i][:, P * g : P * (g + 1)],
-                            rhs=w1_sb[g][:, cols].bitcast(FP8X4),
-                            rhs_scale=w1_plane(g, cols),
-                            start=(g == 0),
-                            stop=(g == PASSES_1 - 1),
-                        )
+        all_passes = list(range(PASSES_1))
+        first, second = all_passes[:3], all_passes[3:]
+        grouped = transpose_x(0, all_passes[:4])
+        quantise_x(0, grouped)
+        permute_planes(0)
+        for g in all_passes[4:]:
+            grouped = transpose_x(0, [g])
+            quantise_x(0, grouped)
+            permute_w1(0, [g - 4])
+        permute_w1(0, all_passes[2:])
+        nc.vector.tensor_copy(out=b1_cols[:], in_=b1_cols_bf16[:])
+        nc.vector.tensor_copy(out=c_f32[:], in_=c_bf16[:])
 
-        def add_b1(i):
-            for half in range(PASSES_2):
-                planes = work.tile([P, PACK, P], F32)
-                nc.vector.tensor_tensor(
-                    out=planes[:],
-                    in0=sums[(i, half)][:].rearrange("n (p t) -> n t p", t=PACK),
-                    in1=b1_planes[:, half, :, :],
-                    op=ALU.add,
-                )
-                pre[(i, half)] = planes
+        layer1(0, 0, True)
+        silu(0, 0)
+        grouped = transpose_x(1, all_passes)
+        quantise_h(0, 0)
+        quantise_x(1, grouped)
+        permute_planes(1)
+        permute_w1(1, all_passes)
 
-        def transpose_h(i):
-            grouped_h = work.tile([P, PASSES_2, P, PACK], BF16, align_bytes=64)
-            for half in range(PASSES_2):
-                ht = ps_h.tile([P, PACK, P], F32, tag="bank")
-                for t in range(PACK):
-                    nc.tensor.transpose(ht[:, t, :], pre[(i, half)][:, t, :], identity[:])
-                nc.scalar.activation(
-                    out=grouped_h[:, half, :, :], in_=ht[:].rearrange("p t n -> p n t"), func=ACT.Silu
-                )
-            codes_h = work.tile([P, PASSES_2 * P], U32, align_bytes=64)
-            scales_h = work.tile([P, PASSES_2 * P], U8, align_bytes=64)
-            nc.vector.quantize_mx(
-                out=codes_h[:].bitcast(FP8X4),
-                scales=scales_h[:],
-                in_=grouped_h[:].rearrange("p g n t -> p (g n t)"),
-            )
-            h_codes[i], h_scales[i] = codes_h, scales_h
-
-        def layer2(tiles):
-            if not tiles:
-                return
-            bank_z = ps_z.tile([P, FIRST_GROUP, H1], F32)
-            for slot, i in enumerate(tiles):
-                z_sums[i] = bank_z[:, slot, :]
-                for g in range(PASSES_2):
-                    nc.tensor.matmul_mx(
-                        out=z_sums[i],
-                        lhsT=h_codes[i][:, P * g : P * (g + 1)].bitcast(FP8X4),
-                        lhsT_scale=h_scales[i][:, P * g : P * (g + 1)],
-                        rhs=w2_sb[:, g, :].bitcast(FP8X4),
-                        rhs_scale=w2_plane(g),
-                        start=(g == 0),
-                        stop=(g == PASSES_2 - 1),
-                    )
-
-        def finish_z(i):
-            nc.vector.tensor_tensor(out=z_sb[:, i, :], in0=z_sums[i], in1=b2_all[:], op=ALU.add)
-            nc.sync.dma_start(out=z_tiles_dram[i], in_=z_sb[:, i, :])
-
-        def transpose_z(i):
-            zt = ps_x.tile([P, Z_HALVES, P], F32, tag="xt")
-            for half in range(Z_HALVES):
-                nc.tensor.transpose(zt[:, half, :], z_sb[:, i, P * half : P * (half + 1)], identity[:])
-            zt_copy = work.tile([P, Z_HALVES, P], F32)
-            nc.scalar.copy(out=zt_copy[:], in_=zt[:])
-            zt_sb[i] = zt_copy
-            z_squares = work.tile([P, H1], F32)
-            nc.scalar.activation(
-                out=z_squares[:], in_=z_sb[:, i, :], func=ACT.Square, accum_out=z_norm[:, i : i + 1]
-            )
-
-        def centroid_products(i):
-            dot = ps_h.tile([P, BANK], F32, tag="bank")
-            for half in range(Z_HALVES):
-                nc.tensor.matmul(
-                    out=dot[:, 0:CENTROIDS_PAD],
-                    lhsT=zt_sb[i][:, half, :],
-                    rhs=ct_minus2[:, half, :],
-                    start=(half == 0),
-                    stop=(half == Z_HALVES - 1),
-                )
-            nc.vector.scalar_tensor_tensor(
-                out=d2_plus1[:, i, :],
-                in0=dot[:, 0:CENTROIDS],
-                scalar=z_norm[:, i : i + 1],
-                in1=c_norm_plus1[:, 0:CENTROIDS],
-                op0=ALU.add,
-                op1=ALU.add,
-            )
-
-        def soft_assignment(i):
-            nc.vector.reciprocal(out=t_sb[:, i, :], in_=d2_plus1[:, i, :])
-            nc.vector.reduce_sum(out=t_sum[:, i : i + 1], in_=t_sb[:, i, :], axis=AXIS.X)
-            nc.vector.reciprocal(out=t_scale[:, i : i + 1], in_=t_sum[:, i : i + 1])
-            nc.vector.tensor_scalar_mul(out=q_sb[:, i, :], in0=t_sb[:, i, :], scalar1=t_scale[:, i : i + 1])
-
-        for i in group(0):
-            transpose_x(i)
+        layer1(1, 0, False)
+        silu(1, 0)
         constants()
-        for a in range(len(groups) + 2):
-            layer1(group(a))
-            layer2(group(a - 1))
-            for i in group(a):
-                add_b1(i)
-            for i in group(a - 1):
-                finish_z(i)
-            for i in group(a - 2):
-                centroid_products(i)
-            for i in group(a + 1):
-                transpose_x(i)
-            for i in group(a):
-                transpose_h(i)
-            for i in group(a - 1):
-                transpose_z(i)
-            for i in group(a - 2):
-                soft_assignment(i)
+        grouped = transpose_x(2, first)
+        quantise_h(1, 0)
+        quantise_x(2, grouped)
+
+        layer1(0, 1, False)
+        silu(0, 1)
+        spread_c_norm()
+        grouped = transpose_x(2, second)
+        quantise_h(0, 1)
+        quantise_x(2, grouped)
+
+        layer1(1, 1, False)
+        silu(1, 1)
+        layer2(0)
+        grouped = transpose_x(3, first)
+        quantise_h(1, 1)
+        finish_z(0)
+        quantise_x(3, grouped)
+
+        layer1(2, 0, False)
+        silu(2, 0)
+        layer2(1)
+        grouped = transpose_x(3, second)
+        group_products(0)
+        quantise_h(2, 0)
+        finish_z(1)
+        quantise_x(3, grouped)
+        soft_assignment(0)
+
+        layer1(2, 1, False)
+        silu(2, 1)
+        group_products(1)
+        quantise_h(2, 1)
+        soft_assignment(1)
+
+        layer1(3, 0, False)
+        silu(3, 0)
+        layer2(2)
+        quantise_h(3, 0)
+        finish_z(2)
+
+        layer1_tile(3, 1, 0)
+        silu_tile(3, 1, 0)
+        interleave_tile(3, 1, 0)
+        quantise_tile(3, 1, 0)
+        group_products(2)
+        soft_assignment(2)
         nc.sync.dma_start(
-            out=out_1.rearrange("(p i) k -> p (i k)", i=TILES), in_=q_sb[:].rearrange("p i k -> p (i k)")
+            out=q_dram[:, 0 : (TILES - PAIR) * CENTROIDS],
+            in_=q_sb[:, 0 : TILES - PAIR, :].rearrange("p i k -> p (i k)"),
+        )
+        layer1_tile(3, 1, 1)
+        silu_tile(3, 1, 1)
+        layer2_tile(3, 0)
+        interleave_tile(3, 1, 1)
+        add_b2_tile(3, 0)
+        quantise_tile(3, 1, 1)
+        hi_tile(3, 0)
+        lo_tile(3, 0)
+        square_tile(3, 0)
+        layer2_tile(3, 1)
+        dot_0 = ps_h.tile([P, CENTROIDS_PAD], F32, tag="bank")
+        products(dot_0[:], zt_hi[(3, 0)], zt_lo[(3, 0)], slice(0, P))
+        hi_tile(3, 1)
+        add_b2_tile(3, 1)
+        lo_tile(3, 1)
+        square_tile(3, 1)
+        dot_1 = ps_h.tile([P, CENTROIDS_PAD], F32, tag="bank")
+        products(dot_1[:], zt_hi[(3, 1)], zt_lo[(3, 1)], slice(0, P))
+        distances(3, 0, dot_0)
+        distances(3, 1, dot_1)
+        normalise(3)
+        nc.sync.dma_start(
+            out=q_dram[:, (TILES - PAIR) * CENTROIDS :],
+            in_=q_sb[:, TILES - PAIR :, :].rearrange("p i k -> p (i k)"),
         )

@@ -47,6 +47,7 @@ def tile_lintrans_pa_kernel(
         w1_pool = ctx.enter_context(tc.tile_pool(name="w1_pool", bufs=PASSES_1 * PASSES_2))
         work = ctx.enter_context(tc.tile_pool(name="work", bufs=4))
         grouped_pool = ctx.enter_context(tc.tile_pool(name="grouped_pool", bufs=8))
+        sorted_pool = ctx.enter_context(tc.tile_pool(name="sorted_pool", bufs=8))
         ps_x = ctx.enter_context(tc.psum_pool(name="ps_x", bufs=3))
         ps_h = ctx.enter_context(tc.psum_pool(name="ps_h", bufs=5))
         ctx.enter_context(tc.manual_schedule())
@@ -141,6 +142,16 @@ def tile_lintrans_pa_kernel(
         x_codes, x_scales, w1, sums, h_raw, h_codes, h_scales = {}, {}, {}, {}, {}, {}, {}
         z_bank, zt_bank, zt_hi, zt_lo, dots = {}, {}, {}, {}, {}
 
+        x_sorted = {}
+
+        def sort_x(a, passes, copy):
+            for g in passes:
+                xs = sorted_pool.tile([P, PAIR, 2, P], F32)
+                words = x_sb[(a, g // CHUNK)][:].rearrange("p i k -> p (i k)").bitcast(F32)
+                words = words.rearrange("p (i c w u) -> p i c w u", i=PAIR, c=CHUNK, u=2)
+                copy(out=xs[:].rearrange("p i u w -> p i w u"), in_=words[:, :, g % CHUNK, :, :])
+                x_sorted[(a, g)] = xs
+
         def transpose_x(a, passes):
             grouped = {}
             for g in passes:
@@ -149,7 +160,10 @@ def tile_lintrans_pa_kernel(
                     words = x_sb[(a, g // CHUNK)][:, i, :].bitcast(F32)
                     first = WORDS * (g % CHUNK)
                     for u in range(2):
-                        nc.tensor.transpose(xt[:, i, u, :], words[:, first + u : first + WORDS : 2], identity[:])
+                        in_ = words[:, first + u : first + WORDS : 2]
+                        if (a, g) in x_sorted:
+                            in_ = x_sorted[(a, g)][:, i, u, :]
+                        nc.tensor.transpose(xt[:, i, u, :], in_, identity[:])
                 out = grouped_pool.tile([P, PAIR, P, PACK], BF16, align_bytes=64)
                 nc.scalar.copy(out=out[:].bitcast(F32), in_=xt[:].rearrange("p i u n -> p i n u"))
                 grouped[g] = out
@@ -454,11 +468,13 @@ def tile_lintrans_pa_kernel(
         permute_planes(1)
         permute_w1(1, all_passes)
 
+        sort_x(2, first, nc.scalar.copy)
         layer1(1, 0, False)
         silu(1, 0)
         constants()
         grouped = transpose_x(2, first)
         quantise_h(1, 0)
+        sort_x(2, second, nc.vector.tensor_copy)
         quantise_x(2, grouped)
 
         layer1(0, 1, False)
@@ -466,6 +482,7 @@ def tile_lintrans_pa_kernel(
         spread_c_norm()
         grouped = transpose_x(2, second)
         quantise_h(0, 1)
+        sort_x(3, first, nc.vector.tensor_copy)
         quantise_x(2, grouped)
 
         layer1(1, 1, False)
@@ -474,6 +491,7 @@ def tile_lintrans_pa_kernel(
         grouped = transpose_x(3, first)
         quantise_h(1, 1)
         finish_z(0)
+        sort_x(3, second, nc.vector.tensor_copy)
         quantise_x(3, grouped)
 
         layer1(2, 0, False)

@@ -28,6 +28,7 @@ PASSES_2 = H0 // K_PASS
 HALF = H0 // PASSES_2
 Z_HALVES = H1 // P
 CENTROIDS_PAD = 32
+LINE = 4
 CHUNK = 2
 
 FLOPS = 2 * TOKENS * D_IN * H0 + 2 * TOKENS * H0 * H1
@@ -148,8 +149,10 @@ def tile_lintrans_pa_kernel(
             for g in passes:
                 xs = sorted_pool.tile([P, PAIR, 2, P], F32)
                 words = x_sb[(a, g // CHUNK)][:].rearrange("p i k -> p (i k)").bitcast(F32)
-                words = words.rearrange("p (i c w u) -> p i c w u", i=PAIR, c=CHUNK, u=2)
-                copy(out=xs[:].rearrange("p i u w -> p i w u"), in_=words[:, :, g % CHUNK, :, :])
+                words = words.rearrange("p (i c b w u) -> p i c b u w", i=PAIR, c=CHUNK, u=2, w=LINE)
+                sorted_view = xs[:].rearrange("p i u (b w) -> p i b u w", w=LINE)
+                for i in range(PAIR):
+                    copy(out=sorted_view[:, i, :, :, :], in_=words[:, i, g % CHUNK, :, :, :])
                 x_sorted[(a, g)] = xs
 
         def transpose_x(a, passes):
@@ -184,16 +187,18 @@ def tile_lintrans_pa_kernel(
         def permute_planes(half):
             for s, planes in enumerate((planes_a, planes_b)):
                 nc.vector.tensor_copy(
-                    out=planes_1[:, s, half, :, :].rearrange("p t m -> p m t"),
-                    in_=planes[:, HALF * half : HALF * (half + 1)].rearrange("p (m t) -> p m t", t=PACK),
+                    out=planes_1[:, s, half, :, :].rearrange("p t (b m) -> p b t m", m=4 * LINE),
+                    in_=planes[:, HALF * half : HALF * (half + 1)].rearrange(
+                        "p (b m t) -> p b t m", m=4 * LINE, t=PACK
+                    ),
                 )
 
         def permute_w1(half, passes):
             for g in passes:
                 permuted = w1_pool.tile([P, PACK, P], U32, align_bytes=64)
                 nc.vector.tensor_copy(
-                    out=permuted[:].bitcast(I32).rearrange("p t m -> p m t"),
-                    in_=w1_raw[(half, g)][:].bitcast(I32).rearrange("p (m t) -> p m t", t=PACK),
+                    out=permuted[:].bitcast(I32).rearrange("p t (b m) -> p b t m", m=LINE),
+                    in_=w1_raw[(half, g)][:].bitcast(I32).rearrange("p (b m t) -> p b t m", m=LINE, t=PACK),
                 )
                 w1[(half, g)] = permuted
 
@@ -250,7 +255,10 @@ def tile_lintrans_pa_kernel(
 
         def interleave_tile(a, half, i):
             grouped = work.tile([P, P, PACK], BF16, align_bytes=64, tag="grouped_tile")
-            nc.vector.tensor_copy(out=grouped[:], in_=h_raw[(a, half, i)][:].rearrange("p t n -> p n t"))
+            nc.vector.tensor_copy(
+                out=grouped[:].rearrange("p (b n) t -> p b t n", n=LINE),
+                in_=h_raw[(a, half, i)][:].rearrange("p t (b n) -> p b t n", n=LINE),
+            )
             h_raw[(a, half, i)] = grouped
 
         def quantise_tile(a, half, i):
@@ -326,8 +334,8 @@ def tile_lintrans_pa_kernel(
             grouped = work.tile([P, PAIR, P, PACK], BF16, align_bytes=64, tag="grouped_h")
             for i in range(PAIR):
                 nc.vector.tensor_copy(
-                    out=grouped[:, i, :, :],
-                    in_=h_raw[(a, half)][:, :, P * i : P * (i + 1)].rearrange("p t n -> p n t"),
+                    out=grouped[:, i, :, :].rearrange("p (b n) t -> p b t n", n=LINE),
+                    in_=h_raw[(a, half)][:, :, P * i : P * (i + 1)].rearrange("p t (b n) -> p b t n", n=LINE),
                 )
             for i in range(PAIR):
                 nc.vector.quantize_mx(

@@ -60,6 +60,8 @@ def tile_lintrans_pa_kernel(
         planes_b = keep.tile([P, H0], U8, align_bytes=64)
         nc.vector.memset(planes_a[:].bitcast(I32), 0)
         nc.vector.memset(planes_b[:].bitcast(I32), 0)
+        planes_2 = keep.tile([P, H1], U8, align_bytes=64)
+        nc.vector.memset(planes_2[:].bitcast(I32), 0)
         identity = keep.tile([P, P], F32)
         make_identity(nc, identity[:])
         c_bf16 = keep.tile([P, H1], BF16)
@@ -70,24 +72,26 @@ def tile_lintrans_pa_kernel(
         nc.gpsimd.memset(ones[:], 1.0)
 
         b1_cols_bf16 = keep.tile([P, PASSES_2, PACK], BF16)
-        nc.scalar.dma_start(out=b1_cols_bf16[:], in_=b1.rearrange("(c p t) -> p c t", c=PASSES_2, t=PACK))
         nc.scalar.activation(out=table_out[:], in_=table_in[:], func=ACT.Silu)
         nc.gpsimd.dma_start(out=c_bf16[0:CENTROIDS, :], in_=clusters)
         nc.gpsimd.dma_start(out=b2_row[0:1, :], in_=b2.rearrange("(o n) -> o n", o=1))
 
         x_sb = {}
 
+        def load_x_chunk(a, c):
+            x_tile = x_pool.tile([P, PAIR, CHUNK * K_PASS], BF16)
+            cols = slice(CHUNK * K_PASS * c, CHUNK * K_PASS * (c + 1))
+            nc.sync.dma_start(out=x_tile[:], in_=x_dram[:, PAIR * a : PAIR * (a + 1), cols])
+            x_sb[(a, c)] = x_tile
+
         def load_x(a):
             for c in range(PASSES_1 // CHUNK):
-                x_tile = x_pool.tile([P, PAIR, CHUNK * K_PASS], BF16)
-                cols = slice(CHUNK * K_PASS * c, CHUNK * K_PASS * (c + 1))
-                nc.sync.dma_start(out=x_tile[:], in_=x_dram[:, PAIR * a : PAIR * (a + 1), cols])
-                x_sb[(a, c)] = x_tile
+                load_x_chunk(a, c)
 
         w1_raw = {}
 
-        def load_w1(half):
-            for g in range(PASSES_1):
+        def load_w1(half, passes):
+            for g in passes:
                 raw = w1_pool.tile([P, HALF], U32, align_bytes=64)
                 words = W1_words[g].rearrange("p n t -> p (n t)")
                 nc.sync.dma_start(
@@ -96,25 +100,26 @@ def tile_lintrans_pa_kernel(
                 )
                 w1_raw[(half, g)] = raw
 
-        load_x(0)
-        for quadrant in range(4):
-            rows = slice(4 * quadrant, 4 * quadrant + 4)
-            first = 32 * quadrant
-            nc.sync.dma_start(
-                out=planes_a[first : first + 16, :].bitcast(I32), in_=W1_scales[0:4, rows, :].bitcast(I32)
-            )
-        for quadrant in range(4):
-            rows = slice(4 * quadrant, 4 * quadrant + 4)
-            first = 32 * quadrant
-            nc.sync.dma_start(
-                out=planes_b[first : first + 8, :].bitcast(I32), in_=W1_scales[4:6, rows, :].bitcast(I32)
-            )
-            nc.sync.dma_start(
-                out=planes_b[first + 8 : first + 16, 0:H1].bitcast(I32), in_=W2_scales[:, rows, :].bitcast(I32)
-            )
-        load_w1(0)
+        def load_scales(planes, scales):
+            for quadrant in range(4):
+                rows = slice(4 * quadrant, 4 * quadrant + 4)
+                start = 32 * quadrant
+                nc.sync.dma_start(
+                    out=planes[start : start + 4 * scales.shape[0], :].bitcast(I32),
+                    in_=scales[:, rows, :].bitcast(I32),
+                )
+
+        load_x_chunk(0, 0)
+        load_x_chunk(0, 1)
+        load_scales(planes_a, W1_scales[0:4])
+        load_x_chunk(0, 2)
+        load_w1(0, (0, 1, 2))
+        load_scales(planes_b, W1_scales[4:6])
+        load_w1(0, (3, 4, 5))
+        nc.sync.dma_start(out=b1_cols_bf16[:], in_=b1.rearrange("(c p t) -> p c t", c=PASSES_2, t=PACK))
         load_x(1)
-        load_w1(1)
+        load_w1(1, range(PASSES_1))
+        load_scales(planes_2, W2_scales)
         w2_sb = keep.tile([P, PASSES_2, H1], U32, align_bytes=64)
         for g in range(PASSES_2):
             nc.sync.dma_start(
@@ -184,8 +189,9 @@ def tile_lintrans_pa_kernel(
                     in_=grouped[g][:].rearrange("p i n t -> p (i n t)"),
                 )
 
-        def permute_planes(half):
-            for s, planes in enumerate((planes_a, planes_b)):
+        def permute_planes(half, which):
+            for s in which:
+                planes = (planes_a, planes_b)[s]
                 nc.vector.tensor_copy(
                     out=planes_1[:, s, half, :, :].rearrange("p t (b m) -> p b t m", m=4 * LINE),
                     in_=planes[:, HALF * half : HALF * (half + 1)].rearrange(
@@ -279,7 +285,7 @@ def tile_lintrans_pa_kernel(
                     lhsT=h_codes[a][:, g, cols].bitcast(FP8X4),
                     lhsT_scale=h_scales[a][:, g, cols],
                     rhs=w2_sb[:, g, :].bitcast(FP8X4),
-                    rhs_scale=planes_b[8 + 4 * g : P, 0:H1],
+                    rhs_scale=planes_2[4 * g : P, 0:H1],
                     start=(g == 0),
                     stop=(g == PASSES_2 - 1),
                 )
@@ -289,7 +295,7 @@ def tile_lintrans_pa_kernel(
                     nc.tensor.matmul_mx(
                         out=zt_bank[(a, i)][:, j, :],
                         lhsT=w2_sb[:, g, rows].bitcast(FP8X4),
-                        lhsT_scale=planes_b[8 + 4 * g : P, rows],
+                        lhsT_scale=planes_2[4 * g : P, rows],
                         rhs=h_codes[a][:, g, cols].bitcast(FP8X4),
                         rhs_scale=h_scales[a][:, g, cols],
                         start=(g == 0),
@@ -354,7 +360,7 @@ def tile_lintrans_pa_kernel(
                         lhsT=h_codes[a][:, g, P * i : P * (i + 1)].bitcast(FP8X4),
                         lhsT_scale=h_scales[a][:, g, P * i : P * (i + 1)],
                         rhs=w2_sb[:, g, :].bitcast(FP8X4),
-                        rhs_scale=planes_b[8 + 4 * g : P, 0:H1],
+                        rhs_scale=planes_2[4 * g : P, 0:H1],
                         start=(g == 0),
                         stop=(g == PASSES_2 - 1),
                     )
@@ -364,7 +370,7 @@ def tile_lintrans_pa_kernel(
                     nc.tensor.matmul_mx(
                         out=zt_bank[a][:, j, :],
                         lhsT=w2_sb[:, g, cols].bitcast(FP8X4),
-                        lhsT_scale=planes_b[8 + 4 * g : P, cols],
+                        lhsT_scale=planes_2[4 * g : P, cols],
                         rhs=h_codes[a][:, g, :].bitcast(FP8X4),
                         rhs_scale=h_scales[a][:, g, :],
                         start=(g == 0),
@@ -459,22 +465,24 @@ def tile_lintrans_pa_kernel(
         first, second = all_passes[:3], all_passes[3:]
         grouped = transpose_x(0, all_passes[:4])
         quantise_x(0, grouped)
-        permute_planes(0)
+        permute_planes(0, [0])
         for g in all_passes[4:]:
             grouped = transpose_x(0, [g])
-            quantise_x(0, grouped)
             permute_w1(0, [g - 4])
-        permute_w1(0, all_passes[2:])
+            quantise_x(0, grouped)
+        permute_w1(0, [2, 3])
+        permute_planes(0, [1])
+        permute_w1(0, [4, 5])
         nc.vector.tensor_copy(out=b1_cols[:], in_=b1_cols_bf16[:])
         nc.vector.tensor_copy(out=c_f32[:], in_=c_bf16[:])
 
         layer1(0, 0, True)
-        silu(0, 0)
         grouped = transpose_x(1, all_passes)
-        quantise_h(0, 0)
+        silu(0, 0)
         quantise_x(1, grouped)
-        permute_planes(1)
+        permute_planes(1, [0, 1])
         permute_w1(1, all_passes)
+        quantise_h(0, 0)
 
         sort_x(2, first, nc.scalar.copy)
         layer1(1, 0, False)

@@ -21,7 +21,6 @@ WORDS = K_PASS // 2
 TOKENS, D_IN, H0, H1, CENTROIDS = 1024, 3072, 1024, 256, 20
 TILES = TOKENS // P
 PAIR = 2
-GROUPS = TILES // PAIR
 GT = PAIR * P
 PASSES_1 = D_IN // K_PASS
 PASSES_2 = H0 // K_PASS
@@ -29,7 +28,6 @@ HALF = H0 // PASSES_2
 Z_HALVES = H1 // P
 CENTROIDS_PAD = 32
 LINE = 4
-CHUNK = 2
 
 FLOPS = 2 * TOKENS * D_IN * H0 + 2 * TOKENS * H0 * H1
 
@@ -38,17 +36,20 @@ def tile_lintrans_pa_kernel(
     tc, x, W1_words, W1_scales, b1, W2_words, W2_scales, b2, clusters, out_0, out_1
 ):
     nc = tc.nc
-    x_dram = x.rearrange("(p i) k -> p i k", i=TILES)
-    q_dram = out_1.rearrange("(p i) k -> p (i k)", i=TILES)
+    x_dram = x.rearrange("(p i) k -> i p k", i=TILES)
     z_dram = out_0.rearrange("(p i) j -> p i j", i=TILES)
+    q_dram = out_1.rearrange("(p i) k -> p (i k)", i=TILES)
+    sets = [[0, 1, 2, 3], [4, 5], [6, 7]]
 
     with ExitStack() as ctx:
         keep = ctx.enter_context(tc.tile_pool(name="keep", bufs=1))
-        x_pool = ctx.enter_context(tc.tile_pool(name="x_pool", bufs=GROUPS * PASSES_1 // CHUNK))
+        x_pool = ctx.enter_context(tc.tile_pool(name="x_pool", bufs=TILES))
+        raw_pool = ctx.enter_context(tc.tile_pool(name="raw_pool", bufs=PASSES_1))
         w1_pool = ctx.enter_context(tc.tile_pool(name="w1_pool", bufs=PASSES_1 * PASSES_2))
+        codes_pool = ctx.enter_context(tc.tile_pool(name="codes_pool", bufs=2))
         work = ctx.enter_context(tc.tile_pool(name="work", bufs=4))
-        grouped_pool = ctx.enter_context(tc.tile_pool(name="grouped_pool", bufs=8))
-        sorted_pool = ctx.enter_context(tc.tile_pool(name="sorted_pool", bufs=8))
+        grouped_pool = ctx.enter_context(tc.tile_pool(name="grouped_pool", bufs=6))
+        sorted_pool = ctx.enter_context(tc.tile_pool(name="sorted_pool", bufs=6))
         ps_x = ctx.enter_context(tc.psum_pool(name="ps_x", bufs=3))
         ps_h = ctx.enter_context(tc.psum_pool(name="ps_h", bufs=5))
         ctx.enter_context(tc.manual_schedule())
@@ -76,29 +77,17 @@ def tile_lintrans_pa_kernel(
         nc.gpsimd.dma_start(out=c_bf16[0:CENTROIDS, :], in_=clusters)
         nc.gpsimd.dma_start(out=b2_row[0:1, :], in_=b2.rearrange("(o n) -> o n", o=1))
 
-        x_sb = {}
+        x_sb, w1_raw = {}, {}
 
-        def load_x_chunk(a, c):
-            x_tile = x_pool.tile([P, PAIR, CHUNK * K_PASS], BF16)
-            cols = slice(CHUNK * K_PASS * c, CHUNK * K_PASS * (c + 1))
-            nc.sync.dma_start(out=x_tile[:], in_=x_dram[:, PAIR * a : PAIR * (a + 1), cols])
-            x_sb[(a, c)] = x_tile
+        def load_x(i):
+            x_tile = x_pool.tile([P, D_IN], BF16)
+            nc.sync.dma_start(out=x_tile[:], in_=x_dram[i])
+            x_sb[i] = x_tile
 
-        def load_x(a):
-            for c in range(PASSES_1 // CHUNK):
-                load_x_chunk(a, c)
-
-        w1_raw = {}
-
-        def load_w1(half, passes):
-            for g in passes:
-                raw = w1_pool.tile([P, HALF], U32, align_bytes=64)
-                words = W1_words[g].rearrange("p n t -> p (n t)")
-                nc.sync.dma_start(
-                    out=raw[:].bitcast(I32),
-                    in_=words[:, PACK * HALF * half : PACK * HALF * (half + 1)].bitcast(I32),
-                )
-                w1_raw[(half, g)] = raw
+        def load_w1(g):
+            raw = raw_pool.tile([P, H0], U32, align_bytes=64)
+            nc.sync.dma_start(out=raw[:].bitcast(I32), in_=W1_words[g].rearrange("p n t -> p (n t)").bitcast(I32))
+            w1_raw[g] = raw
 
         def load_scales(planes, scales):
             for quadrant in range(4):
@@ -109,24 +98,26 @@ def tile_lintrans_pa_kernel(
                     in_=scales[:, rows, :].bitcast(I32),
                 )
 
-        load_x_chunk(0, 0)
-        load_x_chunk(0, 1)
+        for i in (0, 1, 2):
+            load_x(i)
         load_scales(planes_a, W1_scales[0:4])
-        load_x_chunk(0, 2)
-        load_w1(0, (0, 1, 2))
+        load_x(3)
+        for g in (0, 1, 2):
+            load_w1(g)
         load_scales(planes_b, W1_scales[4:6])
-        load_w1(0, (3, 4, 5))
+        for g in (3, 4, 5):
+            load_w1(g)
         nc.sync.dma_start(out=b1_cols_bf16[:], in_=b1.rearrange("(c p t) -> p c t", c=PASSES_2, t=PACK))
-        load_x(1)
-        load_w1(1, range(PASSES_1))
+        for i in (4, 5):
+            load_x(i)
         load_scales(planes_2, W2_scales)
         w2_sb = keep.tile([P, PASSES_2, H1], U32, align_bytes=64)
         for g in range(PASSES_2):
             nc.sync.dma_start(
                 out=w2_sb[:, g, :].bitcast(I32), in_=W2_words[g].rearrange("p n t -> p (n t)").bitcast(I32)
             )
-        for a in range(2, GROUPS):
-            load_x(a)
+        for i in (6, 7):
+            load_x(i)
 
         b1_cols = keep.tile([P, PASSES_2, PACK], F32)
         planes_1 = keep.tile([P, 2, PASSES_2, PACK, P], U8, align_bytes=64)
@@ -145,237 +136,195 @@ def tile_lintrans_pa_kernel(
         t_scale = keep.tile([P, TILES], F32)
         q_sb = keep.tile([P, TILES, CENTROIDS], F32)
 
-        x_codes, x_scales, w1, sums, h_raw, h_codes, h_scales = {}, {}, {}, {}, {}, {}, {}
-        z_bank, zt_bank, zt_hi, zt_lo, dots = {}, {}, {}, {}, {}
+        x_codes, x_scales, x_sorted, w1, sums, h_raw = {}, {}, {}, {}, {}, {}
+        h_codes, h_scales, z_bank, zt_bank, zt_hi, zt_lo, dots = {}, {}, {}, {}, {}, {}, {}
 
-        x_sorted = {}
+        def sort_x(i, copy):
+            for two in range(PASSES_1 // 2):
+                xs = sorted_pool.tile([P, 2, 2, P], F32)
+                words = x_sb[i][:].bitcast(F32)[:, 2 * WORDS * two : 2 * WORDS * (two + 1)]
+                words = words.rearrange("p (s b w u) -> p s b u w", s=2, u=2, w=LINE)
+                sorted_view = xs[:].rearrange("p s u (b w) -> p s b u w", w=LINE)
+                for s in range(2):
+                    copy(out=sorted_view[:, s, :, :, :], in_=words[:, s, :, :, :])
+                x_sorted[(i, two)] = xs
 
-        def sort_x(a, passes, copy):
-            for g in passes:
-                xs = sorted_pool.tile([P, PAIR, 2, P], F32)
-                words = x_sb[(a, g // CHUNK)][:].rearrange("p i k -> p (i k)").bitcast(F32)
-                words = words.rearrange("p (i c b w u) -> p i c b u w", i=PAIR, c=CHUNK, u=2, w=LINE)
-                sorted_view = xs[:].rearrange("p i u (b w) -> p i b u w", w=LINE)
-                for i in range(PAIR):
-                    copy(out=sorted_view[:, i, :, :, :], in_=words[:, i, g % CHUNK, :, :, :])
-                x_sorted[(a, g)] = xs
-
-        def transpose_x(a, passes):
+        def transpose_x(i, twos=range(PASSES_1 // 2)):
             grouped = {}
-            for g in passes:
-                xt = ps_x.tile([P, PAIR, 2, P], F32, tag="xt")
-                for i in range(PAIR):
-                    words = x_sb[(a, g // CHUNK)][:, i, :].bitcast(F32)
-                    first = WORDS * (g % CHUNK)
+            for two in twos:
+                xt = ps_x.tile([P, 2, 2, P], F32, tag="xt")
+                words = x_sb[i][:].bitcast(F32)
+                for s in range(2):
+                    first = WORDS * (2 * two + s)
                     for u in range(2):
                         in_ = words[:, first + u : first + WORDS : 2]
-                        if (a, g) in x_sorted:
-                            in_ = x_sorted[(a, g)][:, i, u, :]
-                        nc.tensor.transpose(xt[:, i, u, :], in_, identity[:])
-                out = grouped_pool.tile([P, PAIR, P, PACK], BF16, align_bytes=64)
-                nc.scalar.copy(out=out[:].bitcast(F32), in_=xt[:].rearrange("p i u n -> p i n u"))
-                grouped[g] = out
+                        if (i, two) in x_sorted:
+                            in_ = x_sorted[(i, two)][:, s, u, :]
+                        nc.tensor.transpose(xt[:, s, u, :], in_, identity[:])
+                out = grouped_pool.tile([P, 2, P, PACK], BF16, align_bytes=64)
+                nc.scalar.copy(out=out[:].bitcast(F32), in_=xt[:].rearrange("p s u n -> p s n u"))
+                grouped[two] = out
             return grouped
 
-        def quantise_x(a, grouped):
+        def quantise_x(a, i, grouped):
+            tiles = sets[a]
             if a not in x_codes:
-                codes = work.tile([P, PASSES_1, GT], U32, align_bytes=64)
-                scales = work.tile([P, PASSES_1, GT], U8, align_bytes=64)
+                codes = codes_pool.tile([P, PASSES_1, len(tiles) * P], U32, align_bytes=64, tag="codes_" + str(len(tiles)), bufs=4 // len(tiles))
+                scales = codes_pool.tile([P, PASSES_1, len(tiles) * P], U8, align_bytes=64, tag="scales_" + str(len(tiles)), bufs=4 // len(tiles))
                 x_codes[a], x_scales[a] = codes, scales
-            for g in grouped:
-                nc.vector.quantize_mx(
-                    out=x_codes[a][:, g, :].bitcast(FP8X4),
-                    scales=x_scales[a][:, g, :],
-                    in_=grouped[g][:].rearrange("p i n t -> p (i n t)"),
-                )
+            cols = slice(P * tiles.index(i), P * (tiles.index(i) + 1))
+            for two in grouped:
+                for s in range(2):
+                    g = 2 * two + s
+                    nc.vector.quantize_mx(
+                        out=x_codes[a][:, g, cols].bitcast(FP8X4),
+                        scales=x_scales[a][:, g, cols],
+                        in_=grouped[two][:, s, :, :].rearrange("p n t -> p (n t)"),
+                    )
 
-        def permute_planes(half, which):
-            for s in which:
-                planes = (planes_a, planes_b)[s]
-                nc.vector.tensor_copy(
-                    out=planes_1[:, s, half, :, :].rearrange("p t (b m) -> p b t m", m=4 * LINE),
-                    in_=planes[:, HALF * half : HALF * (half + 1)].rearrange(
-                        "p (b m t) -> p b t m", m=4 * LINE, t=PACK
-                    ),
-                )
+        def permute_planes(half, s):
+            planes = (planes_a, planes_b)[s]
+            nc.vector.tensor_copy(
+                out=planes_1[:, s, half, :, :].rearrange("p t (b m) -> p b t m", m=4 * LINE),
+                in_=planes[:, HALF * half : HALF * (half + 1)].rearrange("p (b m t) -> p b t m", m=4 * LINE, t=PACK),
+            )
 
         def permute_w1(half, passes):
             for g in passes:
                 permuted = w1_pool.tile([P, PACK, P], U32, align_bytes=64)
+                raw = w1_raw[g][:, HALF * half : HALF * (half + 1)].bitcast(I32)
                 nc.vector.tensor_copy(
                     out=permuted[:].bitcast(I32).rearrange("p t (b m) -> p b t m", m=LINE),
-                    in_=w1_raw[(half, g)][:].bitcast(I32).rearrange("p (b m t) -> p b t m", m=LINE, t=PACK),
+                    in_=raw.rearrange("p (b m t) -> p b t m", m=LINE, t=PACK),
                 )
                 w1[(half, g)] = permuted
 
-        def layer1(a, half, by_pass):
-            def one(t, g):
-                nc.tensor.matmul_mx(
-                    out=sums[(a, half, t)],
-                    lhsT=w1[(half, g)][:, t, :].bitcast(FP8X4),
-                    lhsT_scale=planes_1[4 * (g % 4) : P, g // 4, half, t, :],
-                    rhs=x_codes[a][:, g, :].bitcast(FP8X4),
-                    rhs_scale=x_scales[a][:, g, :],
-                    start=(g == 0),
-                    stop=(g == PASSES_1 - 1),
-                )
+        def pass_1(a, half, t, g, cols, out):
+            nc.tensor.matmul_mx(
+                out=out,
+                lhsT=w1[(half, g)][:, t, :].bitcast(FP8X4),
+                lhsT_scale=planes_1[4 * (g % 4) : P, g // 4, half, t, :],
+                rhs=x_codes[a][:, g, cols].bitcast(FP8X4),
+                rhs_scale=x_scales[a][:, g, cols],
+                start=(g == 0),
+                stop=(g == PASSES_1 - 1),
+            )
 
-            if by_pass:
-                for t in range(PACK):
-                    bank = ps_h.tile([P, 2, GT], F32, tag="bank")
-                    sums[(a, half, t)] = bank[:, 0, :]
-                for g in range(PASSES_1):
-                    for t in range(PACK):
-                        one(t, g)
-                return
+        def layer1_by_pass(a, half):
+            width = P * len(sets[a])
             for t in range(PACK):
-                if t % 2 == 0:
-                    bank = ps_h.tile([P, 2, GT], F32, tag="bank")
-                sums[(a, half, t)] = bank[:, t % 2, :]
+                bank = ps_h.tile([P, width], F32, tag="bank")
+                sums[(a, half, t)] = bank[:]
+            for g in range(PASSES_1):
+                for t in range(PACK):
+                    pass_1(a, half, t, g, slice(0, width), sums[(a, half, t)])
+
+        def layer1(a, half, ts=range(PACK)):
+            width = P * len(sets[a])
+            fit = 512 // width
+            for t in ts:
+                if t % fit == 0:
+                    bank = ps_h.tile([P, fit, width], F32, tag="bank")
+                sums[(a, half, t)] = bank[:, t % fit, :]
                 for g in range(PASSES_1):
-                    one(t, g)
+                    pass_1(a, half, t, g, slice(0, width), sums[(a, half, t)])
 
         def layer1_tile(a, half, i):
+            n = sets[a].index(i)
             for t in range(PACK):
                 if t in (0, PACK - 1):
                     bank = ps_h.tile([P, PACK - 1, P], F32, tag="bank")
-                sums[(a, half, t, i)] = bank[:, t % (PACK - 1), :]
+                sums[(i, half, t)] = bank[:, t % (PACK - 1), :]
                 for g in range(PASSES_1):
-                    nc.tensor.matmul_mx(
-                        out=sums[(a, half, t, i)],
-                        lhsT=w1[(half, g)][:, t, :].bitcast(FP8X4),
-                        lhsT_scale=planes_1[4 * (g % 4) : P, g // 4, half, t, :],
-                        rhs=x_codes[a][:, g, P * i : P * (i + 1)].bitcast(FP8X4),
-                        rhs_scale=x_scales[a][:, g, P * i : P * (i + 1)],
-                        start=(g == 0),
-                        stop=(g == PASSES_1 - 1),
-                    )
+                    pass_1(a, half, t, g, slice(P * n, P * (n + 1)), sums[(i, half, t)])
 
-        def silu_tile(a, half, i):
+        def silu(a, half, ts=range(PACK)):
+            if (a, half) not in h_raw:
+                raw = work.tile([P, PACK, P * len(sets[a])], BF16, align_bytes=64, tag="raw_" + str(len(sets[a])), bufs=2)
+                h_raw[(a, half)] = raw
+            for t in ts:
+                nc.scalar.activation(
+                    out=h_raw[(a, half)][:, t, :],
+                    in_=sums[(a, half, t)],
+                    func=ACT.Silu,
+                    bias=b1_cols[:, half, t : t + 1],
+                )
+
+        def silu_tile(half, i):
             raw = work.tile([P, PACK, P], BF16, align_bytes=64, tag="raw_tile")
             for t in range(PACK):
                 nc.scalar.activation(
-                    out=raw[:, t, :], in_=sums[(a, half, t, i)], func=ACT.Silu, bias=b1_cols[:, half, t : t + 1]
+                    out=raw[:, t, :], in_=sums[(i, half, t)], func=ACT.Silu, bias=b1_cols[:, half, t : t + 1]
                 )
-            h_raw[(a, half, i)] = raw
+            h_raw[(i, half, "tile")] = raw[:]
 
-        def interleave_tile(a, half, i):
-            grouped = work.tile([P, P, PACK], BF16, align_bytes=64, tag="grouped_tile")
+        def interleave(half, i, raw):
+            grouped = work.tile([P, P, PACK], BF16, align_bytes=64, tag="grouped_h")
             nc.vector.tensor_copy(
                 out=grouped[:].rearrange("p (b n) t -> p b t n", n=LINE),
-                in_=h_raw[(a, half, i)][:].rearrange("p t (b n) -> p b t n", n=LINE),
+                in_=raw.rearrange("p t (b n) -> p b t n", n=LINE),
             )
-            h_raw[(a, half, i)] = grouped
+            return grouped
 
-        def quantise_tile(a, half, i):
-            cols = slice(P * i, P * (i + 1))
+        def quantise_tile(half, i, grouped):
+            if i not in h_codes:
+                pair = i // PAIR * PAIR
+                codes = work.tile([P, PASSES_2, GT], U32, align_bytes=64, tag="h_codes")
+                scales = work.tile([P, PASSES_2, GT], U8, align_bytes=64, tag="h_scales")
+                for tile in range(pair, pair + PAIR):
+                    h_codes[tile], h_scales[tile] = codes, scales
+            cols = slice(P * (i % PAIR), P * (i % PAIR + 1))
             nc.vector.quantize_mx(
-                out=h_codes[a][:, half, cols].bitcast(FP8X4),
-                scales=h_scales[a][:, half, cols],
-                in_=h_raw[(a, half, i)][:].rearrange("p n t -> p (n t)"),
+                out=h_codes[i][:, half, cols].bitcast(FP8X4),
+                scales=h_scales[i][:, half, cols],
+                in_=grouped[:].rearrange("p n t -> p (n t)"),
             )
 
-        def layer2_tile(a, i):
-            cols = slice(P * i, P * (i + 1))
-            z_bank[(a, i)] = ps_x.tile([P, H1], F32, tag="xt", name="z_tile")
-            zt_bank[(a, i)] = ps_x.tile([P, Z_HALVES, P], F32, tag="xt", name="zt_tile")
+        def quantise_h(a, half, tiles):
+            raws = {i: h_raw[(a, half)][:, :, P * sets[a].index(i) : P * (sets[a].index(i) + 1)] for i in tiles}
+            grouped = {i: interleave(half, i, raws[i]) for i in tiles}
+            for i in tiles:
+                quantise_tile(half, i, grouped[i])
+
+        def z_sums(i, out):
+            cols = slice(P * (i % PAIR), P * (i % PAIR + 1))
             for g in range(PASSES_2):
                 nc.tensor.matmul_mx(
-                    out=z_bank[(a, i)][:],
-                    lhsT=h_codes[a][:, g, cols].bitcast(FP8X4),
-                    lhsT_scale=h_scales[a][:, g, cols],
+                    out=out,
+                    lhsT=h_codes[i][:, g, cols].bitcast(FP8X4),
+                    lhsT_scale=h_scales[i][:, g, cols],
                     rhs=w2_sb[:, g, :].bitcast(FP8X4),
                     rhs_scale=planes_2[4 * g : P, 0:H1],
                     start=(g == 0),
                     stop=(g == PASSES_2 - 1),
                 )
+
+        def zt_sums(i, cols, bank):
             for j in range(Z_HALVES):
                 rows = slice(P * j, P * (j + 1))
                 for g in range(PASSES_2):
                     nc.tensor.matmul_mx(
-                        out=zt_bank[(a, i)][:, j, :],
+                        out=bank[:, j, :],
                         lhsT=w2_sb[:, g, rows].bitcast(FP8X4),
                         lhsT_scale=planes_2[4 * g : P, rows],
-                        rhs=h_codes[a][:, g, cols].bitcast(FP8X4),
-                        rhs_scale=h_scales[a][:, g, cols],
+                        rhs=h_codes[i][:, g, cols].bitcast(FP8X4),
+                        rhs_scale=h_scales[i][:, g, cols],
                         start=(g == 0),
                         stop=(g == PASSES_2 - 1),
                     )
-
-        def add_b2_tile(a, i):
-            tile = PAIR * a + i
-            nc.vector.tensor_tensor(out=z_sb[:, tile, :], in0=z_bank[(a, i)][:], in1=b2_all[:, 0, :], op=ALU.add)
-            nc.sync.dma_start(out=z_dram[:, tile, :], in_=z_sb[:, tile, :])
-
-        def hi_tile(a, i):
-            hi = work.tile([P, Z_HALVES, P], BF16, tag="hi_tile")
-            nc.scalar.copy(out=hi[:], in_=zt_bank[(a, i)][:])
-            zt_hi[(a, i)] = hi
-
-        def lo_tile(a, i):
-            lo = work.tile([P, Z_HALVES, P], BF16, tag="lo_tile")
-            nc.vector.tensor_tensor(out=lo[:], in0=zt_bank[(a, i)][:], in1=zt_hi[(a, i)][:], op=ALU.subtract)
-            zt_lo[(a, i)] = lo
-
-        def square_tile(a, i):
-            tile = PAIR * a + i
-            z_squares = work.tile([P, H1], F32)
-            nc.scalar.activation(
-                out=z_squares[:], in_=z_sb[:, tile, :], func=ACT.Square, accum_out=z_norm[:, tile : tile + 1]
-            )
-
-        def silu(a, half):
-            raw = work.tile([P, PACK, GT], BF16, align_bytes=64)
-            for t in range(PACK):
-                nc.scalar.activation(
-                    out=raw[:, t, :], in_=sums[(a, half, t)], func=ACT.Silu, bias=b1_cols[:, half, t : t + 1]
-                )
-            h_raw[(a, half)] = raw
-
-        def quantise_h(a, half):
-            if a not in h_codes:
-                codes = work.tile([P, PASSES_2, GT], U32, align_bytes=64, tag="h_codes")
-                scales = work.tile([P, PASSES_2, GT], U8, align_bytes=64, tag="h_scales")
-                h_codes[a], h_scales[a] = codes, scales
-            grouped = work.tile([P, PAIR, P, PACK], BF16, align_bytes=64, tag="grouped_h")
-            for i in range(PAIR):
-                nc.vector.tensor_copy(
-                    out=grouped[:, i, :, :].rearrange("p (b n) t -> p b t n", n=LINE),
-                    in_=h_raw[(a, half)][:, :, P * i : P * (i + 1)].rearrange("p t (b n) -> p b t n", n=LINE),
-                )
-            for i in range(PAIR):
-                nc.vector.quantize_mx(
-                    out=h_codes[a][:, half, P * i : P * (i + 1)].bitcast(FP8X4),
-                    scales=h_scales[a][:, half, P * i : P * (i + 1)],
-                    in_=grouped[:, i, :, :].rearrange("p n t -> p (n t)"),
-                )
 
         def layer2(a):
-            z_bank[a] = ps_h.tile([P, PAIR, H1], F32, tag="bank", name="z_sums")
-            zt_bank[a] = ps_h.tile([P, Z_HALVES, GT], F32, tag="bank", name="zt_sums")
-            for i in range(PAIR):
-                for g in range(PASSES_2):
-                    nc.tensor.matmul_mx(
-                        out=z_bank[a][:, i, :],
-                        lhsT=h_codes[a][:, g, P * i : P * (i + 1)].bitcast(FP8X4),
-                        lhsT_scale=h_scales[a][:, g, P * i : P * (i + 1)],
-                        rhs=w2_sb[:, g, :].bitcast(FP8X4),
-                        rhs_scale=planes_2[4 * g : P, 0:H1],
-                        start=(g == 0),
-                        stop=(g == PASSES_2 - 1),
-                    )
-            for j in range(Z_HALVES):
-                cols = slice(P * j, P * (j + 1))
-                for g in range(PASSES_2):
-                    nc.tensor.matmul_mx(
-                        out=zt_bank[a][:, j, :],
-                        lhsT=w2_sb[:, g, cols].bitcast(FP8X4),
-                        lhsT_scale=planes_2[4 * g : P, cols],
-                        rhs=h_codes[a][:, g, :].bitcast(FP8X4),
-                        rhs_scale=h_scales[a][:, g, :],
-                        start=(g == 0),
-                        stop=(g == PASSES_2 - 1),
-                    )
+            z_bank[a] = ps_h.tile([P, PAIR, H1], F32, tag="bank", name="z_sums_bank")
+            zt_bank[a] = ps_h.tile([P, Z_HALVES, GT], F32, tag="bank", name="zt_sums_bank")
+            for n in range(PAIR):
+                z_sums(PAIR * a + n, z_bank[a][:, n, :])
+            zt_sums(PAIR * a, slice(0, GT), zt_bank[a])
+
+        def layer2_tile(i):
+            z_bank[("tile", i)] = ps_x.tile([P, H1], F32, tag="xt", name="z_tile")
+            zt_bank[("tile", i)] = ps_x.tile([P, Z_HALVES, P], F32, tag="xt", name="zt_tile")
+            z_sums(i, z_bank[("tile", i)][:])
+            zt_sums(i, slice(P * (i % PAIR), P * (i % PAIR + 1)), zt_bank[("tile", i)])
 
         def finish_z(a):
             tiles = slice(PAIR * a, PAIR * (a + 1))
@@ -386,11 +335,26 @@ def tile_lintrans_pa_kernel(
             lo = work.tile([P, Z_HALVES, GT], BF16, tag="zt_lo")
             nc.vector.tensor_tensor(out=lo[:], in0=zt_bank[a][:], in1=hi[:], op=ALU.subtract)
             zt_hi[a], zt_lo[a] = hi, lo
-            for i in range(PAIR * a, PAIR * (a + 1)):
-                z_squares = work.tile([P, H1], F32)
-                nc.scalar.activation(
-                    out=z_squares[:], in_=z_sb[:, i, :], func=ACT.Square, accum_out=z_norm[:, i : i + 1]
-                )
+
+        def add_b2_tile(i):
+            nc.vector.tensor_tensor(out=z_sb[:, i, :], in0=z_bank[("tile", i)][:], in1=b2_all[:, 0, :], op=ALU.add)
+            nc.sync.dma_start(out=z_dram[:, i, :], in_=z_sb[:, i, :])
+
+        def hi_tile(i):
+            hi = work.tile([P, Z_HALVES, P], BF16, tag="hi_tile")
+            nc.scalar.copy(out=hi[:], in_=zt_bank[("tile", i)][:])
+            zt_hi[("tile", i)] = hi
+
+        def lo_tile(i):
+            lo = work.tile([P, Z_HALVES, P], BF16, tag="lo_tile")
+            nc.vector.tensor_tensor(
+                out=lo[:], in0=zt_bank[("tile", i)][:], in1=zt_hi[("tile", i)][:], op=ALU.subtract
+            )
+            zt_lo[("tile", i)] = lo
+
+        def square(i):
+            z_squares = work.tile([P, H1], F32)
+            nc.scalar.activation(out=z_squares[:], in_=z_sb[:, i, :], func=ACT.Square, accum_out=z_norm[:, i : i + 1])
 
         def products(out, hi, lo, cols):
             parts = [(part, j) for part in (hi, lo) for j in range(Z_HALVES)]
@@ -403,12 +367,17 @@ def tile_lintrans_pa_kernel(
                     stop=(n == len(parts) - 1),
                 )
 
-        def distances(a, i, dot):
-            tile = PAIR * a + i
+        def pair_products(a):
+            bank = ps_h.tile([P, PAIR, CENTROIDS_PAD], F32, tag="bank", name="dots")
+            for n in range(PAIR):
+                products(bank[:, n, :], zt_hi[a], zt_lo[a], slice(P * n, P * (n + 1)))
+            dots[a] = bank
+
+        def distances(i, dot):
             nc.vector.scalar_tensor_tensor(
-                out=d2_plus1[:, tile, :],
+                out=d2_plus1[:, i, :],
                 in0=dot[:, 0:CENTROIDS],
-                scalar=z_norm[:, tile : tile + 1],
+                scalar=z_norm[:, i : i + 1],
                 in1=c_norm_plus1[:, 0:CENTROIDS],
                 op0=ALU.add,
                 op1=ALU.add,
@@ -419,26 +388,18 @@ def tile_lintrans_pa_kernel(
             nc.vector.reciprocal(out=t_sb[:, tiles, :], in_=d2_plus1[:, tiles, :])
             nc.vector.reduce_sum(out=t_sum[:, tiles], in_=t_sb[:, tiles, :], axis=AXIS.X)
             nc.vector.reciprocal(out=t_scale[:, tiles], in_=t_sum[:, tiles])
-            for tile in range(PAIR * a, PAIR * (a + 1)):
-                nc.vector.tensor_scalar_mul(
-                    out=q_sb[:, tile, :], in0=t_sb[:, tile, :], scalar1=t_scale[:, tile : tile + 1]
-                )
-
-        def group_products(a):
-            bank = ps_h.tile([P, PAIR, CENTROIDS_PAD], F32, tag="bank", name="dots")
-            for i in range(PAIR):
-                products(bank[:, i, :], zt_hi[a], zt_lo[a], slice(P * i, P * (i + 1)))
-            dots[a] = bank
+            for i in range(PAIR * a, PAIR * (a + 1)):
+                nc.vector.tensor_scalar_mul(out=q_sb[:, i, :], in0=t_sb[:, i, :], scalar1=t_scale[:, i : i + 1])
 
         def soft_assignment(a):
-            for i in range(PAIR):
-                distances(a, i, dots[a][:, i, :])
+            for n in range(PAIR):
+                distances(PAIR * a + n, dots[a][:, n, :])
             normalise(a)
 
         def constants():
             spread = ps_h.tile([P, PAIR, H1], F32, tag="bank")
-            for i in range(PAIR):
-                nc.tensor.matmul(out=spread[:, i, :], lhsT=ones[:], rhs=b2_row[:], start=True, stop=True)
+            for n in range(PAIR):
+                nc.tensor.matmul(out=spread[:, n, :], lhsT=ones[:], rhs=b2_row[:], start=True, stop=True)
             ct = ps_h.tile([P, Z_HALVES, P], F32, tag="bank")
             for j in range(Z_HALVES):
                 nc.tensor.transpose(ct[:, j, :], c_f32[:, P * j : P * (j + 1)], identity[:])
@@ -461,107 +422,109 @@ def tile_lintrans_pa_kernel(
             )
             nc.vector.tensor_scalar_add(out=c_norm_plus1[:], in0=norms[:, 0:CENTROIDS_PAD], scalar1=1.0)
 
-        all_passes = list(range(PASSES_1))
-        first, second = all_passes[:3], all_passes[3:]
-        grouped = transpose_x(0, all_passes[:4])
-        quantise_x(0, grouped)
-        permute_planes(0, [0])
-        for g in all_passes[4:]:
-            grouped = transpose_x(0, [g])
-            permute_w1(0, [g - 4])
-            quantise_x(0, grouped)
-        permute_w1(0, [2, 3])
-        permute_planes(0, [1])
-        permute_w1(0, [4, 5])
-        nc.vector.tensor_copy(out=b1_cols[:], in_=b1_cols_bf16[:])
+        for i in (0, 1, 2):
+            grouped = transpose_x(i)
+            quantise_x(0, i, grouped)
+        permute_planes(0, 0)
+        for two in range(PASSES_1 // 2):
+            grouped = transpose_x(3, [two])
+            quantise_x(0, 3, grouped)
+            permute_w1(0, [two])
+        permute_planes(0, 1)
         nc.vector.tensor_copy(out=c_f32[:], in_=c_bf16[:])
+        for g in (3, 4, 5):
+            permute_w1(0, [g])
+            permute_w1(1, [g - 3])
+        permute_planes(1, 0)
+        permute_planes(1, 1)
+        nc.vector.tensor_copy(out=b1_cols[:], in_=b1_cols_bf16[:])
+        permute_w1(1, [3, 4, 5])
 
-        layer1(0, 0, True)
-        grouped = transpose_x(1, all_passes)
+        layer1_by_pass(0, 0)
         silu(0, 0)
-        quantise_x(1, grouped)
-        permute_planes(1, [0, 1])
-        permute_w1(1, all_passes)
-        quantise_h(0, 0)
-
-        sort_x(2, first, nc.scalar.copy)
-        layer1(1, 0, False)
-        silu(1, 0)
+        sort_x(4, nc.vector.tensor_copy)
+        layer1(0, 1, (0,))
+        grouped = transpose_x(4)
         constants()
-        grouped = transpose_x(2, first)
-        quantise_h(1, 0)
-        sort_x(2, second, nc.vector.tensor_copy)
-        quantise_x(2, grouped)
-
-        layer1(0, 1, False)
-        silu(0, 1)
+        silu(0, 1, (0,))
+        sort_x(5, nc.vector.tensor_copy)
+        quantise_x(1, 4, grouped)
+        layer1(0, 1, (1, 2))
         spread_c_norm()
-        grouped = transpose_x(2, second)
-        quantise_h(0, 1)
-        sort_x(3, first, nc.vector.tensor_copy)
-        quantise_x(2, grouped)
+        grouped = transpose_x(5)
+        silu(0, 1, (1, 2))
+        sort_x(6, nc.vector.tensor_copy)
+        quantise_x(1, 5, grouped)
+        quantise_h(0, 0, (0, 1))
+        layer1(0, 1, (3,))
+        grouped = transpose_x(6)
+        silu(0, 1, (3,))
+        sort_x(7, nc.vector.tensor_copy)
+        quantise_h(0, 0, (2, 3))
+        quantise_x(2, 6, grouped)
 
-        layer1(1, 1, False)
-        silu(1, 1)
+        layer1(1, 0)
+        quantise_h(0, 1, (0, 1))
+        silu(1, 0)
         layer2(0)
-        grouped = transpose_x(3, first)
-        quantise_h(1, 1)
+        grouped = transpose_x(7)
+        quantise_h(0, 1, (2, 3))
         finish_z(0)
-        sort_x(3, second, nc.vector.tensor_copy)
-        quantise_x(3, grouped)
+        quantise_x(2, 7, grouped)
+        quantise_h(1, 0, (4, 5))
 
-        layer1(2, 0, False)
-        silu(2, 0)
+        layer1(1, 1)
+        silu(1, 1)
+        square(0)
+        square(1)
         layer2(1)
-        grouped = transpose_x(3, second)
-        group_products(0)
-        quantise_h(2, 0)
+        pair_products(0)
+        quantise_h(1, 1, (4, 5))
         finish_z(1)
-        quantise_x(3, grouped)
         soft_assignment(0)
 
-        layer1(2, 1, False)
-        silu(2, 1)
-        group_products(1)
-        quantise_h(2, 1)
+        layer1(2, 0)
+        silu(2, 0)
+        square(2)
+        square(3)
+        layer2(2)
+        pair_products(1)
+        quantise_h(2, 0, (6, 7))
+        finish_z(2)
         soft_assignment(1)
 
-        layer1(3, 0, False)
-        silu(3, 0)
-        layer2(2)
-        quantise_h(3, 0)
-        finish_z(2)
-
-        layer1_tile(3, 1, 0)
-        silu_tile(3, 1, 0)
-        interleave_tile(3, 1, 0)
-        quantise_tile(3, 1, 0)
-        group_products(2)
+        layer1_tile(2, 1, 6)
+        silu_tile(1, 6)
+        square(4)
+        square(5)
+        grouped = interleave(1, 6, h_raw[(6, 1, "tile")])
+        quantise_tile(1, 6, grouped)
+        pair_products(2)
         soft_assignment(2)
         nc.sync.dma_start(
             out=q_dram[:, 0 : (TILES - PAIR) * CENTROIDS],
             in_=q_sb[:, 0 : TILES - PAIR, :].rearrange("p i k -> p (i k)"),
         )
-        layer1_tile(3, 1, 1)
-        silu_tile(3, 1, 1)
-        layer2_tile(3, 0)
-        interleave_tile(3, 1, 1)
-        add_b2_tile(3, 0)
-        quantise_tile(3, 1, 1)
-        hi_tile(3, 0)
-        lo_tile(3, 0)
-        square_tile(3, 0)
-        layer2_tile(3, 1)
-        dot_0 = ps_h.tile([P, CENTROIDS_PAD], F32, tag="bank")
-        products(dot_0[:], zt_hi[(3, 0)], zt_lo[(3, 0)], slice(0, P))
-        hi_tile(3, 1)
-        add_b2_tile(3, 1)
-        lo_tile(3, 1)
-        square_tile(3, 1)
-        dot_1 = ps_h.tile([P, CENTROIDS_PAD], F32, tag="bank")
-        products(dot_1[:], zt_hi[(3, 1)], zt_lo[(3, 1)], slice(0, P))
-        distances(3, 0, dot_0)
-        distances(3, 1, dot_1)
+        layer1_tile(2, 1, 7)
+        silu_tile(1, 7)
+        layer2_tile(6)
+        grouped = interleave(1, 7, h_raw[(7, 1, "tile")])
+        add_b2_tile(6)
+        quantise_tile(1, 7, grouped)
+        hi_tile(6)
+        lo_tile(6)
+        square(6)
+        layer2_tile(7)
+        dot_6 = ps_h.tile([P, CENTROIDS_PAD], F32, tag="bank")
+        products(dot_6[:], zt_hi[("tile", 6)], zt_lo[("tile", 6)], slice(0, P))
+        hi_tile(7)
+        add_b2_tile(7)
+        lo_tile(7)
+        square(7)
+        dot_7 = ps_h.tile([P, CENTROIDS_PAD], F32, tag="bank")
+        products(dot_7[:], zt_hi[("tile", 7)], zt_lo[("tile", 7)], slice(0, P))
+        distances(6, dot_6)
+        distances(7, dot_7)
         normalise(3)
         nc.sync.dma_start(
             out=q_dram[:, (TILES - PAIR) * CENTROIDS :],

@@ -286,9 +286,9 @@ def tile_lintrans_pa_kernel(
             for i in tiles:
                 quantise_tile(half, i, grouped[i])
 
-        def z_sums(i, out):
+        def z_sums(i, out, passes=range(PASSES_2)):
             cols = slice(P * (i % PAIR), P * (i % PAIR + 1))
-            for g in range(PASSES_2):
+            for g in passes:
                 nc.tensor.matmul_mx(
                     out=out,
                     lhsT=h_codes[i][:, g, cols].bitcast(FP8X4),
@@ -299,12 +299,12 @@ def tile_lintrans_pa_kernel(
                     stop=(g == PASSES_2 - 1),
                 )
 
-        def zt_sums(i, cols, bank):
+        def zt_sums(i, cols, outs, passes=range(PASSES_2)):
             for j in range(Z_HALVES):
                 rows = slice(P * j, P * (j + 1))
-                for g in range(PASSES_2):
+                for g in passes:
                     nc.tensor.matmul_mx(
-                        out=bank[:, j, :],
+                        out=outs[j],
                         lhsT=w2_sb[:, g, rows].bitcast(FP8X4),
                         lhsT_scale=planes_2[4 * g : P, rows],
                         rhs=h_codes[i][:, g, cols].bitcast(FP8X4),
@@ -318,13 +318,22 @@ def tile_lintrans_pa_kernel(
             zt_bank[a] = ps_h.tile([P, Z_HALVES, GT], F32, tag="bank", name="zt_sums_bank")
             for n in range(PAIR):
                 z_sums(PAIR * a + n, z_bank[a][:, n, :])
-            zt_sums(PAIR * a, slice(0, GT), zt_bank[a])
+            zt_sums(PAIR * a, slice(0, GT), [zt_bank[a][:, j, :] for j in range(Z_HALVES)])
 
-        def layer2_tile(i):
-            z_bank[("tile", i)] = ps_x.tile([P, H1], F32, tag="xt", name="z_tile")
-            zt_bank[("tile", i)] = ps_x.tile([P, Z_HALVES, P], F32, tag="xt", name="zt_tile")
-            z_sums(i, z_bank[("tile", i)][:])
-            zt_sums(i, slice(P * (i % PAIR), P * (i % PAIR + 1)), zt_bank[("tile", i)])
+        def open_layer2(i):
+            pool, tag = (ps_x, "xt") if i % PAIR == 0 else (ps_h, "bank")
+            zt_bank[("tile", i)] = []
+            for j in range(Z_HALVES):
+                zt_half = pool.tile([P, P], F32, tag=tag)
+                zt_bank[("tile", i)].append(zt_half[:])
+            z_tile = pool.tile([P, H1], F32, tag=tag)
+            z_bank[("tile", i)] = z_tile
+            zt_sums(i, slice(P * (i % PAIR), P * (i % PAIR + 1)), zt_bank[("tile", i)], (0,))
+            z_sums(i, z_tile[:], (0,))
+
+        def close_layer2(i):
+            zt_sums(i, slice(P * (i % PAIR), P * (i % PAIR + 1)), zt_bank[("tile", i)], (1,))
+            z_sums(i, z_bank[("tile", i)][:], (1,))
 
         def finish_z(a):
             tiles = slice(PAIR * a, PAIR * (a + 1))
@@ -342,14 +351,16 @@ def tile_lintrans_pa_kernel(
 
         def hi_tile(i):
             hi = work.tile([P, Z_HALVES, P], BF16, tag="hi_tile")
-            nc.scalar.copy(out=hi[:], in_=zt_bank[("tile", i)][:])
+            for j in range(Z_HALVES):
+                nc.scalar.copy(out=hi[:, j, :], in_=zt_bank[("tile", i)][j])
             zt_hi[("tile", i)] = hi
 
         def lo_tile(i):
             lo = work.tile([P, Z_HALVES, P], BF16, tag="lo_tile")
-            nc.vector.tensor_tensor(
-                out=lo[:], in0=zt_bank[("tile", i)][:], in1=zt_hi[("tile", i)][:], op=ALU.subtract
-            )
+            for j in range(Z_HALVES):
+                nc.vector.tensor_tensor(
+                    out=lo[:, j, :], in0=zt_bank[("tile", i)][j], in1=zt_hi[("tile", i)][:, j, :], op=ALU.subtract
+                )
             zt_lo[("tile", i)] = lo
 
         def square(i):
@@ -373,6 +384,11 @@ def tile_lintrans_pa_kernel(
                 products(bank[:, n, :], zt_hi[a], zt_lo[a], slice(P * n, P * (n + 1)))
             dots[a] = bank
 
+        def products_tile(i):
+            dot = ps_h.tile([P, CENTROIDS_PAD], F32, tag="bank")
+            products(dot[:], zt_hi[("tile", i)], zt_lo[("tile", i)], slice(0, P))
+            dots[("tile", i)] = dot
+
         def distances(i, dot):
             nc.vector.scalar_tensor_tensor(
                 out=d2_plus1[:, i, :],
@@ -387,6 +403,9 @@ def tile_lintrans_pa_kernel(
             tiles = slice(PAIR * a, PAIR * (a + 1))
             nc.vector.reciprocal(out=t_sb[:, tiles, :], in_=d2_plus1[:, tiles, :])
             nc.vector.reduce_sum(out=t_sum[:, tiles], in_=t_sb[:, tiles, :], axis=AXIS.X)
+
+        def scale_q(a):
+            tiles = slice(PAIR * a, PAIR * (a + 1))
             nc.vector.reciprocal(out=t_scale[:, tiles], in_=t_sum[:, tiles])
             for i in range(PAIR * a, PAIR * (a + 1)):
                 nc.vector.tensor_scalar_mul(out=q_sb[:, i, :], in0=t_sb[:, i, :], scalar1=t_scale[:, i : i + 1])
@@ -395,20 +414,27 @@ def tile_lintrans_pa_kernel(
             for n in range(PAIR):
                 distances(PAIR * a + n, dots[a][:, n, :])
             normalise(a)
+            scale_q(a)
 
         def constants():
-            spread = ps_h.tile([P, PAIR, H1], F32, tag="bank")
+            spread = ps_x.tile([P, PAIR, H1], F32, tag="xt")
             for n in range(PAIR):
                 nc.tensor.matmul(out=spread[:, n, :], lhsT=ones[:], rhs=b2_row[:], start=True, stop=True)
-            ct = ps_h.tile([P, Z_HALVES, P], F32, tag="bank")
+            ct = ps_x.tile([P, Z_HALVES, P], F32, tag="xt")
             for j in range(Z_HALVES):
                 nc.tensor.transpose(ct[:, j, :], c_f32[:, P * j : P * (j + 1)], identity[:])
             nc.vector.tensor_copy(out=b2_all[:], in_=spread[:])
             nc.vector.tensor_scalar_mul(out=ct_minus2[:], in0=ct[:, :, 0:CENTROIDS_PAD], scalar1=-2.0)
+
+        def c_less_2b2():
             nc.vector.scalar_tensor_tensor(
                 out=c_less[:], in0=b2_all[:, 0, :], scalar=-2.0, in1=c_f32[:], op0=ALU.mult, op1=ALU.add
             )
+
+        def c_norms():
             nc.vector.tensor_tensor(out=c_prod[:], in0=c_less[:], in1=c_f32[:], op=ALU.mult)
+
+        def c_norms_sum():
             nc.vector.reduce_sum(out=c_norm[:], in_=c_prod[:], axis=AXIS.X)
 
         def spread_c_norm():
@@ -425,32 +451,41 @@ def tile_lintrans_pa_kernel(
         for i in (0, 1, 2):
             grouped = transpose_x(i)
             quantise_x(0, i, grouped)
+            if i == 0:
+                nc.vector.tensor_copy(out=c_f32[:], in_=c_bf16[:])
         permute_planes(0, 0)
         for two in range(PASSES_1 // 2):
             grouped = transpose_x(3, [two])
             quantise_x(0, 3, grouped)
             permute_w1(0, [two])
+        constants()
         permute_planes(0, 1)
-        nc.vector.tensor_copy(out=c_f32[:], in_=c_bf16[:])
-        for g in (3, 4, 5):
-            permute_w1(0, [g])
-            permute_w1(1, [g - 3])
+        permute_w1(0, [3])
         permute_planes(1, 0)
+        permute_w1(1, [0])
+        permute_w1(0, [4])
         permute_planes(1, 1)
+        permute_w1(1, [1])
+        permute_w1(0, [5])
+        permute_w1(1, [2])
         nc.vector.tensor_copy(out=b1_cols[:], in_=b1_cols_bf16[:])
-        permute_w1(1, [3, 4, 5])
+        c_less_2b2()
+        permute_w1(1, [3])
+        c_norms()
+        permute_w1(1, [4])
+        c_norms_sum()
+        permute_w1(1, [5])
 
         layer1_by_pass(0, 0)
         silu(0, 0)
         sort_x(4, nc.vector.tensor_copy)
         layer1(0, 1, (0,))
+        spread_c_norm()
         grouped = transpose_x(4)
-        constants()
         silu(0, 1, (0,))
         sort_x(5, nc.vector.tensor_copy)
         quantise_x(1, 4, grouped)
         layer1(0, 1, (1, 2))
-        spread_c_norm()
         grouped = transpose_x(5)
         silu(0, 1, (1, 2))
         sort_x(6, nc.vector.tensor_copy)
@@ -500,32 +535,36 @@ def tile_lintrans_pa_kernel(
         grouped = interleave(1, 6, h_raw[(6, 1, "tile")])
         quantise_tile(1, 6, grouped)
         pair_products(2)
-        soft_assignment(2)
+        distances(4, dots[2][:, 0, :])
+        distances(5, dots[2][:, 1, :])
+        normalise(2)
+        layer1_tile(2, 1, 7)
+        silu_tile(1, 7)
+        open_layer2(6)
+        close_layer2(6)
+        open_layer2(7)
+        grouped = interleave(1, 7, h_raw[(7, 1, "tile")])
+        quantise_tile(1, 7, grouped)
+        hi_tile(6)
+        add_b2_tile(6)
+        lo_tile(6)
+        close_layer2(7)
+        products_tile(6)
+        hi_tile(7)
+        square(6)
+        add_b2_tile(7)
+        lo_tile(7)
+        square(7)
+        products_tile(7)
+        distances(6, dots[("tile", 6)])
+        scale_q(2)
         nc.sync.dma_start(
             out=q_dram[:, 0 : (TILES - PAIR) * CENTROIDS],
             in_=q_sb[:, 0 : TILES - PAIR, :].rearrange("p i k -> p (i k)"),
         )
-        layer1_tile(2, 1, 7)
-        silu_tile(1, 7)
-        layer2_tile(6)
-        grouped = interleave(1, 7, h_raw[(7, 1, "tile")])
-        add_b2_tile(6)
-        quantise_tile(1, 7, grouped)
-        hi_tile(6)
-        lo_tile(6)
-        square(6)
-        layer2_tile(7)
-        dot_6 = ps_h.tile([P, CENTROIDS_PAD], F32, tag="bank")
-        products(dot_6[:], zt_hi[("tile", 6)], zt_lo[("tile", 6)], slice(0, P))
-        hi_tile(7)
-        add_b2_tile(7)
-        lo_tile(7)
-        square(7)
-        dot_7 = ps_h.tile([P, CENTROIDS_PAD], F32, tag="bank")
-        products(dot_7[:], zt_hi[("tile", 7)], zt_lo[("tile", 7)], slice(0, P))
-        distances(6, dot_6)
-        distances(7, dot_7)
+        distances(7, dots[("tile", 7)])
         normalise(3)
+        scale_q(3)
         nc.sync.dma_start(
             out=q_dram[:, (TILES - PAIR) * CENTROIDS :],
             in_=q_sb[:, TILES - PAIR :, :].rearrange("p i k -> p (i k)"),

@@ -378,11 +378,13 @@ def tile_lintrans_pa_kernel(
                     stop=(n == len(parts) - 1),
                 )
 
-        def pair_products(a):
-            bank = ps_h.tile([P, PAIR, CENTROIDS_PAD], F32, tag="bank", name="dots")
-            for n in range(PAIR):
-                products(bank[:, n, :], zt_hi[a], zt_lo[a], slice(P * n, P * (n + 1)))
-            dots[a] = bank
+        def pair_products(pairs):
+            bank = ps_x.tile([P, TILES, CENTROIDS_PAD], F32, tag="xt", name="dots")
+            for a in pairs:
+                for n in range(PAIR):
+                    i = PAIR * a + n
+                    products(bank[:, i, :], zt_hi[a], zt_lo[a], slice(P * n, P * (n + 1)))
+                    dots[i] = bank[:, i, :]
 
         def products_tile(i):
             dot = ps_h.tile([P, CENTROIDS_PAD], F32, tag="bank")
@@ -399,22 +401,18 @@ def tile_lintrans_pa_kernel(
                 op1=ALU.add,
             )
 
-        def normalise(a):
-            tiles = slice(PAIR * a, PAIR * (a + 1))
+        def invert_d2(tiles):
             nc.vector.reciprocal(out=t_sb[:, tiles, :], in_=d2_plus1[:, tiles, :])
+
+        def sum_t(tiles):
             nc.vector.reduce_sum(out=t_sum[:, tiles], in_=t_sb[:, tiles, :], axis=AXIS.X)
 
-        def scale_q(a):
-            tiles = slice(PAIR * a, PAIR * (a + 1))
+        def invert_sum(tiles):
             nc.vector.reciprocal(out=t_scale[:, tiles], in_=t_sum[:, tiles])
-            for i in range(PAIR * a, PAIR * (a + 1)):
-                nc.vector.tensor_scalar_mul(out=q_sb[:, i, :], in0=t_sb[:, i, :], scalar1=t_scale[:, i : i + 1])
 
-        def soft_assignment(a):
-            for n in range(PAIR):
-                distances(PAIR * a + n, dots[a][:, n, :])
-            normalise(a)
-            scale_q(a)
+        def scale_q(tiles):
+            for i in range(tiles.start, tiles.stop):
+                nc.vector.tensor_scalar_mul(out=q_sb[:, i, :], in0=t_sb[:, i, :], scalar1=t_scale[:, i : i + 1])
 
         def constants():
             spread = ps_x.tile([P, PAIR, H1], F32, tag="xt")
@@ -438,7 +436,7 @@ def tile_lintrans_pa_kernel(
             nc.vector.reduce_sum(out=c_norm[:], in_=c_prod[:], axis=AXIS.X)
 
         def spread_c_norm():
-            norms = ps_h.tile([P, P], F32, tag="bank")
+            norms = ps_x.tile([P, P], F32, tag="xt")
             nc.tensor.matmul(
                 out=norms[:, 0:CENTROIDS_PAD],
                 lhsT=c_norm[:, 0:1].to_broadcast([P, P]),
@@ -480,7 +478,6 @@ def tile_lintrans_pa_kernel(
         silu(0, 0)
         sort_x(4, nc.vector.tensor_copy)
         layer1(0, 1, (0,))
-        spread_c_norm()
         grouped = transpose_x(4)
         silu(0, 1, (0,))
         sort_x(5, nc.vector.tensor_copy)
@@ -513,31 +510,33 @@ def tile_lintrans_pa_kernel(
         square(0)
         square(1)
         layer2(1)
-        pair_products(0)
         quantise_h(1, 1, (4, 5))
         finish_z(1)
-        soft_assignment(0)
 
         layer1(2, 0)
         silu(2, 0)
         square(2)
         square(3)
         layer2(2)
-        pair_products(1)
+        spread_c_norm()
+        pair_products((0, 1))
         quantise_h(2, 0, (6, 7))
         finish_z(2)
-        soft_assignment(1)
+        done = slice(0, 4)
+        for i in range(4):
+            distances(i, dots[i])
+        invert_d2(done)
+        sum_t(done)
 
         layer1_tile(2, 1, 6)
         silu_tile(1, 6)
         square(4)
         square(5)
         grouped = interleave(1, 6, h_raw[(6, 1, "tile")])
+        invert_sum(done)
         quantise_tile(1, 6, grouped)
-        pair_products(2)
-        distances(4, dots[2][:, 0, :])
-        distances(5, dots[2][:, 1, :])
-        normalise(2)
+        scale_q(done)
+        nc.sync.dma_start(out=q_dram[:, 0 : 4 * CENTROIDS], in_=q_sb[:, 0:4, :].rearrange("p i k -> p (i k)"))
         layer1_tile(2, 1, 7)
         silu_tile(1, 7)
         open_layer2(6)
@@ -549,6 +548,7 @@ def tile_lintrans_pa_kernel(
         add_b2_tile(6)
         lo_tile(6)
         close_layer2(7)
+        pair_products((2,))
         products_tile(6)
         hi_tile(7)
         square(6)
@@ -556,16 +556,18 @@ def tile_lintrans_pa_kernel(
         lo_tile(7)
         square(7)
         products_tile(7)
-        distances(6, dots[("tile", 6)])
-        scale_q(2)
-        nc.sync.dma_start(
-            out=q_dram[:, 0 : (TILES - PAIR) * CENTROIDS],
-            in_=q_sb[:, 0 : TILES - PAIR, :].rearrange("p i k -> p (i k)"),
-        )
+        for i in (4, 5, 6):
+            distances(i, dots[i] if i < 6 else dots[("tile", i)])
+        early, last = slice(4, 7), slice(7, 8)
+        invert_d2(early)
         distances(7, dots[("tile", 7)])
-        normalise(3)
-        scale_q(3)
+        sum_t(early)
+        invert_d2(last)
+        invert_sum(early)
+        sum_t(last)
+        scale_q(early)
+        invert_sum(last)
+        scale_q(last)
         nc.sync.dma_start(
-            out=q_dram[:, (TILES - PAIR) * CENTROIDS :],
-            in_=q_sb[:, TILES - PAIR :, :].rearrange("p i k -> p (i k)"),
+            out=q_dram[:, 4 * CENTROIDS :], in_=q_sb[:, 4:TILES, :].rearrange("p i k -> p (i k)")
         )

from contextlib import ExitStack

import concourse.mybir as mybir
from concourse.masks import make_identity

F32 = mybir.dt.float32
BF16 = mybir.dt.bfloat16
I32 = mybir.dt.int32
U32 = mybir.dt.uint32
U8 = mybir.dt.uint8
FP8X4 = mybir.dt.float8_e4m3fn_x4
ACT = mybir.ActivationFunctionType
ALU = mybir.AluOpType
AXIS = mybir.AxisListType

P = 128
PACK = 4
K_PASS = P * PACK
WORDS = K_PASS // 2

TOKENS, D_IN, H0, H1, CENTROIDS = 1024, 3072, 1024, 256, 20
TILES = TOKENS // P
PAIR = 2
GT = PAIR * P
PASSES_1 = D_IN // K_PASS
PASSES_2 = H0 // K_PASS
HALF = H0 // PASSES_2
Z_HALVES = H1 // P
CENTROIDS_PAD = 32
LINE = 4

FLOPS = 2 * TOKENS * D_IN * H0 + 2 * TOKENS * H0 * H1


def tile_lintrans_pa_kernel(
    tc, x, W1_words, W1_scales, b1, W2_words, W2_scales, b2, clusters, out_0, out_1
):
    nc = tc.nc
    x_dram = x.rearrange("(p i) k -> i p k", i=TILES)
    z_dram = out_0.rearrange("(p i) j -> p i j", i=TILES)
    q_dram = out_1.rearrange("(p i) k -> p (i k)", i=TILES)
    sets = [[0, 1, 2, 3], [4, 5], [6, 7]]

    with ExitStack() as ctx:
        keep = ctx.enter_context(tc.tile_pool(name="keep", bufs=1))
        x_pool = ctx.enter_context(tc.tile_pool(name="x_pool", bufs=TILES))
        raw_pool = ctx.enter_context(tc.tile_pool(name="raw_pool", bufs=PASSES_1))
        w1_pool = ctx.enter_context(tc.tile_pool(name="w1_pool", bufs=PASSES_1 * PASSES_2))
        codes_pool = ctx.enter_context(tc.tile_pool(name="codes_pool", bufs=2))
        work = ctx.enter_context(tc.tile_pool(name="work", bufs=4))
        grouped_pool = ctx.enter_context(tc.tile_pool(name="grouped_pool", bufs=6))
        sorted_pool = ctx.enter_context(tc.tile_pool(name="sorted_pool", bufs=6))
        ps_x = ctx.enter_context(tc.psum_pool(name="ps_x", bufs=3))
        ps_h = ctx.enter_context(tc.psum_pool(name="ps_h", bufs=5))
        ctx.enter_context(tc.manual_schedule())

        table_in = keep.tile([P, 1], F32)
        table_out = keep.tile([P, 1], F32)
        nc.vector.memset(table_in[:], 0.0)
        planes_a = keep.tile([P, H0], U8, align_bytes=64)
        planes_b = keep.tile([P, H0], U8, align_bytes=64)
        nc.vector.memset(planes_a[:].bitcast(I32), 0)
        nc.vector.memset(planes_b[:].bitcast(I32), 0)
        planes_2 = keep.tile([P, H1], U8, align_bytes=64)
        nc.vector.memset(planes_2[:].bitcast(I32), 0)
        identity = keep.tile([P, P], F32)
        make_identity(nc, identity[:])
        c_bf16 = keep.tile([P, H1], BF16)
        nc.gpsimd.memset(c_bf16[:], 0.0)
        b2_row = keep.tile([P, H1], BF16)
        nc.gpsimd.memset(b2_row[:], 0.0)
        ones = keep.tile([P, P], BF16)
        nc.gpsimd.memset(ones[:], 1.0)

        b1_cols_bf16 = keep.tile([P, PASSES_2, PACK], BF16)
        nc.scalar.activation(out=table_out[:], in_=table_in[:], func=ACT.Silu)
        nc.gpsimd.dma_start(out=c_bf16[0:CENTROIDS, :], in_=clusters)
        nc.gpsimd.dma_start(out=b2_row[0:1, :], in_=b2.rearrange("(o n) -> o n", o=1))

        x_sb, w1_raw = {}, {}

        def load_x(i):
            x_tile = x_pool.tile([P, D_IN], BF16)
            nc.sync.dma_start(out=x_tile[:], in_=x_dram[i])
            x_sb[i] = x_tile

        def load_w1(g):
            raw = raw_pool.tile([P, H0], U32, align_bytes=64)
            nc.sync.dma_start(out=raw[:].bitcast(I32), in_=W1_words[g].rearrange("p n t -> p (n t)").bitcast(I32))
            w1_raw[g] = raw

        def load_scales(planes, scales):
            for quadrant in range(4):
                rows = slice(4 * quadrant, 4 * quadrant + 4)
                start = 32 * quadrant
                nc.sync.dma_start(
                    out=planes[start : start + 4 * scales.shape[0], :].bitcast(I32),
                    in_=scales[:, rows, :].bitcast(I32),
                )

        for i in (0, 1, 2):
            load_x(i)
        load_scales(planes_a, W1_scales[0:4])
        load_x(3)
        for g in (0, 1, 2):
            load_w1(g)
        load_scales(planes_b, W1_scales[4:6])
        for g in (3, 4, 5):
            load_w1(g)
        nc.sync.dma_start(out=b1_cols_bf16[:], in_=b1.rearrange("(c p t) -> p c t", c=PASSES_2, t=PACK))
        for i in (4, 5):
            load_x(i)
        load_scales(planes_2, W2_scales)
        w2_sb = keep.tile([P, PASSES_2, H1], U32, align_bytes=64)
        for g in range(PASSES_2):
            nc.sync.dma_start(
                out=w2_sb[:, g, :].bitcast(I32), in_=W2_words[g].rearrange("p n t -> p (n t)").bitcast(I32)
            )
        for i in (6, 7):
            load_x(i)

        b1_cols = keep.tile([P, PASSES_2, PACK], F32)
        planes_1 = keep.tile([P, 2, PASSES_2, PACK, P], U8, align_bytes=64)
        b2_all = keep.tile([P, PAIR, H1], F32)
        c_f32 = keep.tile([P, H1], F32)
        c_less = keep.tile([P, H1], F32)
        c_prod = keep.tile([P, H1], F32)
        c_norm = keep.tile([P, 1], F32)
        ct_minus2 = keep.tile([P, Z_HALVES, CENTROIDS_PAD], BF16)
        c_norm_plus1 = keep.tile([P, CENTROIDS_PAD], F32)
        z_sb = keep.tile([P, TILES, H1], F32)
        z_norm = keep.tile([P, TILES], F32)
        d2_plus1 = keep.tile([P, TILES, CENTROIDS], F32)
        t_sb = keep.tile([P, TILES, CENTROIDS], F32)
        t_sum = keep.tile([P, TILES], F32)
        t_scale = keep.tile([P, TILES], F32)
        q_sb = keep.tile([P, TILES, CENTROIDS], F32)

        x_codes, x_scales, x_sorted, w1, sums, h_raw = {}, {}, {}, {}, {}, {}
        h_codes, h_scales, z_bank, zt_bank, zt_hi, zt_lo, dots = {}, {}, {}, {}, {}, {}, {}

        def sort_x(i, copy):
            for two in range(PASSES_1 // 2):
                xs = sorted_pool.tile([P, 2, 2, P], F32)
                words = x_sb[i][:].bitcast(F32)[:, 2 * WORDS * two : 2 * WORDS * (two + 1)]
                words = words.rearrange("p (s b w u) -> p s b u w", s=2, u=2, w=LINE)
                sorted_view = xs[:].rearrange("p s u (b w) -> p s b u w", w=LINE)
                for s in range(2):
                    copy(out=sorted_view[:, s, :, :, :], in_=words[:, s, :, :, :])
                x_sorted[(i, two)] = xs

        def transpose_x(i, twos=range(PASSES_1 // 2)):
            grouped = {}
            for two in twos:
                xt = ps_x.tile([P, 2, 2, P], F32, tag="xt")
                words = x_sb[i][:].bitcast(F32)
                for s in range(2):
                    first = WORDS * (2 * two + s)
                    for u in range(2):
                        in_ = words[:, first + u : first + WORDS : 2]
                        if (i, two) in x_sorted:
                            in_ = x_sorted[(i, two)][:, s, u, :]
                        nc.tensor.transpose(xt[:, s, u, :], in_, identity[:])
                out = grouped_pool.tile([P, 2, P, PACK], BF16, align_bytes=64)
                nc.scalar.copy(out=out[:].bitcast(F32), in_=xt[:].rearrange("p s u n -> p s n u"))
                grouped[two] = out
            return grouped

        def quantise_x(a, i, grouped):
            tiles = sets[a]
            if a not in x_codes:
                codes = codes_pool.tile([P, PASSES_1, len(tiles) * P], U32, align_bytes=64, tag="codes_" + str(len(tiles)), bufs=4 // len(tiles))
                scales = codes_pool.tile([P, PASSES_1, len(tiles) * P], U8, align_bytes=64, tag="scales_" + str(len(tiles)), bufs=4 // len(tiles))
                x_codes[a], x_scales[a] = codes, scales
            cols = slice(P * tiles.index(i), P * (tiles.index(i) + 1))
            for two in grouped:
                for s in range(2):
                    g = 2 * two + s
                    nc.vector.quantize_mx(
                        out=x_codes[a][:, g, cols].bitcast(FP8X4),
                        scales=x_scales[a][:, g, cols],
                        in_=grouped[two][:, s, :, :].rearrange("p n t -> p (n t)"),
                    )

        def permute_planes(half, s):
            planes = (planes_a, planes_b)[s]
            nc.vector.tensor_copy(
                out=planes_1[:, s, half, :, :].rearrange("p t (b m) -> p b t m", m=4 * LINE),
                in_=planes[:, HALF * half : HALF * (half + 1)].rearrange("p (b m t) -> p b t m", m=4 * LINE, t=PACK),
            )

        def permute_w1(half, passes):
            for g in passes:
                permuted = w1_pool.tile([P, PACK, P], U32, align_bytes=64)
                raw = w1_raw[g][:, HALF * half : HALF * (half + 1)].bitcast(I32)
                nc.vector.tensor_copy(
                    out=permuted[:].bitcast(I32).rearrange("p t (b m) -> p b t m", m=LINE),
                    in_=raw.rearrange("p (b m t) -> p b t m", m=LINE, t=PACK),
                )
                w1[(half, g)] = permuted

        def pass_1(a, half, t, g, cols, out):
            nc.tensor.matmul_mx(
                out=out,
                lhsT=w1[(half, g)][:, t, :].bitcast(FP8X4),
                lhsT_scale=planes_1[4 * (g % 4) : P, g // 4, half, t, :],
                rhs=x_codes[a][:, g, cols].bitcast(FP8X4),
                rhs_scale=x_scales[a][:, g, cols],
                start=(g == 0),
                stop=(g == PASSES_1 - 1),
            )

        def layer1_by_pass(a, half):
            width = P * len(sets[a])
            for t in range(PACK):
                bank = ps_h.tile([P, width], F32, tag="bank")
                sums[(a, half, t)] = bank[:]
            for g in range(PASSES_1):
                for t in range(PACK):
                    pass_1(a, half, t, g, slice(0, width), sums[(a, half, t)])

        def layer1(a, half, ts=range(PACK)):
            width = P * len(sets[a])
            fit = 512 // width
            for t in ts:
                if t % fit == 0:
                    bank = ps_h.tile([P, fit, width], F32, tag="bank")
                sums[(a, half, t)] = bank[:, t % fit, :]
                for g in range(PASSES_1):
                    pass_1(a, half, t, g, slice(0, width), sums[(a, half, t)])

        def layer1_tile(a, half, i):
            n = sets[a].index(i)
            for t in range(PACK):
                if t in (0, PACK - 1):
                    bank = ps_h.tile([P, PACK - 1, P], F32, tag="bank")
                sums[(i, half, t)] = bank[:, t % (PACK - 1), :]
                for g in range(PASSES_1):
                    pass_1(a, half, t, g, slice(P * n, P * (n + 1)), sums[(i, half, t)])

        def silu(a, half, ts=range(PACK)):
            if (a, half) not in h_raw:
                raw = work.tile([P, PACK, P * len(sets[a])], BF16, align_bytes=64, tag="raw_" + str(len(sets[a])), bufs=2)
                h_raw[(a, half)] = raw
            for t in ts:
                nc.scalar.activation(
                    out=h_raw[(a, half)][:, t, :],
                    in_=sums[(a, half, t)],
                    func=ACT.Silu,
                    bias=b1_cols[:, half, t : t + 1],
                )

        def silu_tile(half, i):
            raw = work.tile([P, PACK, P], BF16, align_bytes=64, tag="raw_tile")
            for t in range(PACK):
                nc.scalar.activation(
                    out=raw[:, t, :], in_=sums[(i, half, t)], func=ACT.Silu, bias=b1_cols[:, half, t : t + 1]
                )
            h_raw[(i, half, "tile")] = raw[:]

        def interleave(half, i, raw):
            grouped = work.tile([P, P, PACK], BF16, align_bytes=64, tag="grouped_h")
            nc.vector.tensor_copy(
                out=grouped[:].rearrange("p (b n) t -> p b t n", n=LINE),
                in_=raw.rearrange("p t (b n) -> p b t n", n=LINE),
            )
            return grouped

        def quantise_tile(half, i, grouped):
            if i not in h_codes:
                pair = i // PAIR * PAIR
                codes = work.tile([P, PASSES_2, GT], U32, align_bytes=64, tag="h_codes")
                scales = work.tile([P, PASSES_2, GT], U8, align_bytes=64, tag="h_scales")
                for tile in range(pair, pair + PAIR):
                    h_codes[tile], h_scales[tile] = codes, scales
            cols = slice(P * (i % PAIR), P * (i % PAIR + 1))
            nc.vector.quantize_mx(
                out=h_codes[i][:, half, cols].bitcast(FP8X4),
                scales=h_scales[i][:, half, cols],
                in_=grouped[:].rearrange("p n t -> p (n t)"),
            )

        def quantise_h(a, half, tiles):
            raws = {i: h_raw[(a, half)][:, :, P * sets[a].index(i) : P * (sets[a].index(i) + 1)] for i in tiles}
            grouped = {i: interleave(half, i, raws[i]) for i in tiles}
            for i in tiles:
                quantise_tile(half, i, grouped[i])

        def z_sums(i, out, passes=range(PASSES_2)):
            cols = slice(P * (i % PAIR), P * (i % PAIR + 1))
            for g in passes:
                nc.tensor.matmul_mx(
                    out=out,
                    lhsT=h_codes[i][:, g, cols].bitcast(FP8X4),
                    lhsT_scale=h_scales[i][:, g, cols],
                    rhs=w2_sb[:, g, :].bitcast(FP8X4),
                    rhs_scale=planes_2[4 * g : P, 0:H1],
                    start=(g == 0),
                    stop=(g == PASSES_2 - 1),
                )

        def zt_sums(i, cols, outs, passes=range(PASSES_2)):
            for j in range(Z_HALVES):
                rows = slice(P * j, P * (j + 1))
                for g in passes:
                    nc.tensor.matmul_mx(
                        out=outs[j],
                        lhsT=w2_sb[:, g, rows].bitcast(FP8X4),
                        lhsT_scale=planes_2[4 * g : P, rows],
                        rhs=h_codes[i][:, g, cols].bitcast(FP8X4),
                        rhs_scale=h_scales[i][:, g, cols],
                        start=(g == 0),
                        stop=(g == PASSES_2 - 1),
                    )

        def layer2(a):
            z_bank[a] = ps_h.tile([P, PAIR, H1], F32, tag="bank", name="z_sums_bank")
            zt_bank[a] = ps_h.tile([P, Z_HALVES, GT], F32, tag="bank", name="zt_sums_bank")
            for n in range(PAIR):
                z_sums(PAIR * a + n, z_bank[a][:, n, :])
            zt_sums(PAIR * a, slice(0, GT), [zt_bank[a][:, j, :] for j in range(Z_HALVES)])

        def open_layer2(i):
            pool, tag = (ps_x, "xt") if i % PAIR == 0 else (ps_h, "bank")
            zt_bank[("tile", i)] = []
            for j in range(Z_HALVES):
                zt_half = pool.tile([P, P], F32, tag=tag)
                zt_bank[("tile", i)].append(zt_half[:])
            z_tile = pool.tile([P, H1], F32, tag=tag)
            z_bank[("tile", i)] = z_tile
            zt_sums(i, slice(P * (i % PAIR), P * (i % PAIR + 1)), zt_bank[("tile", i)], (0,))
            z_sums(i, z_tile[:], (0,))

        def close_layer2(i):
            zt_sums(i, slice(P * (i % PAIR), P * (i % PAIR + 1)), zt_bank[("tile", i)], (1,))
            z_sums(i, z_bank[("tile", i)][:], (1,))

        def finish_z(a):
            tiles = slice(PAIR * a, PAIR * (a + 1))
            nc.vector.tensor_tensor(out=z_sb[:, tiles, :], in0=z_bank[a][:], in1=b2_all[:], op=ALU.add)
            nc.sync.dma_start(out=z_dram[:, tiles, :], in_=z_sb[:, tiles, :])
            hi = work.tile([P, Z_HALVES, GT], BF16, tag="zt_hi")
            nc.scalar.copy(out=hi[:], in_=zt_bank[a][:])
            lo = work.tile([P, Z_HALVES, GT], BF16, tag="zt_lo")
            nc.vector.tensor_tensor(out=lo[:], in0=zt_bank[a][:], in1=hi[:], op=ALU.subtract)
            zt_hi[a], zt_lo[a] = hi, lo

        def add_b2_tile(i):
            nc.vector.tensor_tensor(out=z_sb[:, i, :], in0=z_bank[("tile", i)][:], in1=b2_all[:, 0, :], op=ALU.add)
            nc.sync.dma_start(out=z_dram[:, i, :], in_=z_sb[:, i, :])

        def hi_tile(i):
            hi = work.tile([P, Z_HALVES, P], BF16, tag="hi_tile")
            for j in range(Z_HALVES):
                nc.scalar.copy(out=hi[:, j, :], in_=zt_bank[("tile", i)][j])
            zt_hi[("tile", i)] = hi

        def lo_tile(i):
            lo = work.tile([P, Z_HALVES, P], BF16, tag="lo_tile")
            for j in range(Z_HALVES):
                nc.vector.tensor_tensor(
                    out=lo[:, j, :], in0=zt_bank[("tile", i)][j], in1=zt_hi[("tile", i)][:, j, :], op=ALU.subtract
                )
            zt_lo[("tile", i)] = lo

        def square(i):
            z_squares = work.tile([P, H1], F32)
            nc.scalar.activation(out=z_squares[:], in_=z_sb[:, i, :], func=ACT.Square, accum_out=z_norm[:, i : i + 1])

        def products(out, hi, lo, cols):
            parts = [(part, j) for part in (hi, lo) for j in range(Z_HALVES)]
            for n, (part, j) in enumerate(parts):
                nc.tensor.matmul(
                    out=out,
                    lhsT=part[:, j, cols],
                    rhs=ct_minus2[:, j, :],
                    start=(n == 0),
                    stop=(n == len(parts) - 1),
                )

        def pair_products(pairs):
            bank = ps_x.tile([P, TILES, CENTROIDS_PAD], F32, tag="xt", name="dots")
            for a in pairs:
                for n in range(PAIR):
                    i = PAIR * a + n
                    products(bank[:, i, :], zt_hi[a], zt_lo[a], slice(P * n, P * (n + 1)))
                    dots[i] = bank[:, i, :]

        def products_tile(i):
            dot = ps_h.tile([P, CENTROIDS_PAD], F32, tag="bank")
            products(dot[:], zt_hi[("tile", i)], zt_lo[("tile", i)], slice(0, P))
            dots[("tile", i)] = dot

        def distances(i, dot):
            nc.vector.scalar_tensor_tensor(
                out=d2_plus1[:, i, :],
                in0=dot[:, 0:CENTROIDS],
                scalar=z_norm[:, i : i + 1],
                in1=c_norm_plus1[:, 0:CENTROIDS],
                op0=ALU.add,
                op1=ALU.add,
            )

        def invert_d2(tiles):
            nc.vector.reciprocal(out=t_sb[:, tiles, :], in_=d2_plus1[:, tiles, :])

        def sum_t(tiles):
            nc.vector.reduce_sum(out=t_sum[:, tiles], in_=t_sb[:, tiles, :], axis=AXIS.X)

        def invert_sum(tiles):
            nc.vector.reciprocal(out=t_scale[:, tiles], in_=t_sum[:, tiles])

        def scale_q(tiles):
            for i in range(tiles.start, tiles.stop):
                nc.vector.tensor_scalar_mul(out=q_sb[:, i, :], in0=t_sb[:, i, :], scalar1=t_scale[:, i : i + 1])

        def constants():
            spread = ps_x.tile([P, PAIR, H1], F32, tag="xt")
            for n in range(PAIR):
                nc.tensor.matmul(out=spread[:, n, :], lhsT=ones[:], rhs=b2_row[:], start=True, stop=True)
            ct = ps_x.tile([P, Z_HALVES, P], F32, tag="xt")
            for j in range(Z_HALVES):
                nc.tensor.transpose(ct[:, j, :], c_f32[:, P * j : P * (j + 1)], identity[:])
            nc.vector.tensor_copy(out=b2_all[:], in_=spread[:])
            nc.vector.tensor_scalar_mul(out=ct_minus2[:], in0=ct[:, :, 0:CENTROIDS_PAD], scalar1=-2.0)

        def c_less_2b2():
            nc.vector.scalar_tensor_tensor(
                out=c_less[:], in0=b2_all[:, 0, :], scalar=-2.0, in1=c_f32[:], op0=ALU.mult, op1=ALU.add
            )

        def c_norms():
            nc.vector.tensor_tensor(out=c_prod[:], in0=c_less[:], in1=c_f32[:], op=ALU.mult)

        def c_norms_sum():
            nc.vector.reduce_sum(out=c_norm[:], in_=c_prod[:], axis=AXIS.X)

        def spread_c_norm():
            norms = ps_x.tile([P, P], F32, tag="xt")
            nc.tensor.matmul(
                out=norms[:, 0:CENTROIDS_PAD],
                lhsT=c_norm[:, 0:1].to_broadcast([P, P]),
                rhs=identity[:, 0:CENTROIDS_PAD],
                start=True,
                stop=True,
            )
            nc.vector.tensor_scalar_add(out=c_norm_plus1[:], in0=norms[:, 0:CENTROIDS_PAD], scalar1=1.0)

        for i in (0, 1, 2):
            grouped = transpose_x(i)
            quantise_x(0, i, grouped)
            if i == 0:
                nc.vector.tensor_copy(out=c_f32[:], in_=c_bf16[:])
        permute_planes(0, 0)
        for two in range(PASSES_1 // 2):
            grouped = transpose_x(3, [two])
            quantise_x(0, 3, grouped)
            permute_w1(0, [two])
        constants()
        permute_planes(0, 1)
        permute_w1(0, [3])
        permute_planes(1, 0)
        permute_w1(1, [0])
        permute_w1(0, [4])
        permute_planes(1, 1)
        permute_w1(1, [1])
        permute_w1(0, [5])
        permute_w1(1, [2])
        nc.vector.tensor_copy(out=b1_cols[:], in_=b1_cols_bf16[:])
        c_less_2b2()
        permute_w1(1, [3])
        c_norms()
        permute_w1(1, [4])
        c_norms_sum()
        permute_w1(1, [5])

        layer1_by_pass(0, 0)
        silu(0, 0)
        sort_x(4, nc.vector.tensor_copy)
        layer1(0, 1, (0,))
        grouped = transpose_x(4)
        silu(0, 1, (0,))
        sort_x(5, nc.vector.tensor_copy)
        quantise_x(1, 4, grouped)
        layer1(0, 1, (1, 2))
        grouped = transpose_x(5)
        silu(0, 1, (1, 2))
        sort_x(6, nc.vector.tensor_copy)
        quantise_x(1, 5, grouped)
        quantise_h(0, 0, (0, 1))
        layer1(0, 1, (3,))
        grouped = transpose_x(6)
        silu(0, 1, (3,))
        sort_x(7, nc.vector.tensor_copy)
        quantise_h(0, 0, (2, 3))
        quantise_x(2, 6, grouped)

        layer1(1, 0)
        quantise_h(0, 1, (0, 1))
        silu(1, 0)
        layer2(0)
        grouped = transpose_x(7)
        quantise_h(0, 1, (2, 3))
        finish_z(0)
        quantise_x(2, 7, grouped)
        quantise_h(1, 0, (4, 5))

        layer1(1, 1)
        silu(1, 1)
        square(0)
        square(1)
        layer2(1)
        quantise_h(1, 1, (4, 5))
        finish_z(1)

        layer1(2, 0)
        silu(2, 0)
        square(2)
        square(3)
        layer2(2)
        spread_c_norm()
        pair_products((0, 1))
        quantise_h(2, 0, (6, 7))
        finish_z(2)
        done = slice(0, 4)
        for i in range(4):
            distances(i, dots[i])
        invert_d2(done)
        sum_t(done)

        layer1_tile(2, 1, 6)
        silu_tile(1, 6)
        square(4)
        square(5)
        grouped = interleave(1, 6, h_raw[(6, 1, "tile")])
        invert_sum(done)
        quantise_tile(1, 6, grouped)
        scale_q(done)
        nc.sync.dma_start(out=q_dram[:, 0 : 4 * CENTROIDS], in_=q_sb[:, 0:4, :].rearrange("p i k -> p (i k)"))
        layer1_tile(2, 1, 7)
        silu_tile(1, 7)
        open_layer2(6)
        close_layer2(6)
        open_layer2(7)
        grouped = interleave(1, 7, h_raw[(7, 1, "tile")])
        quantise_tile(1, 7, grouped)
        hi_tile(6)
        add_b2_tile(6)
        lo_tile(6)
        close_layer2(7)
        pair_products((2,))
        products_tile(6)
        hi_tile(7)
        square(6)
        add_b2_tile(7)
        lo_tile(7)
        square(7)
        products_tile(7)
        for i in (4, 5, 6):
            distances(i, dots[i] if i < 6 else dots[("tile", i)])
        early, last = slice(4, 7), slice(7, 8)
        invert_d2(early)
        distances(7, dots[("tile", 7)])
        sum_t(early)
        invert_d2(last)
        invert_sum(early)
        sum_t(last)
        scale_q(early)
        invert_sum(last)
        scale_q(last)
        nc.sync.dma_start(
            out=q_dram[:, 4 * CENTROIDS :], in_=q_sb[:, 4:TILES, :].rearrange("p i k -> p (i k)")
        )
